import numpy as np
import ml_dtypes


def mxq(x, axis, fmt="e4m3"):
    dtype, down = {"e4m3": (ml_dtypes.float8_e4m3fn, 7), "e5m2": (ml_dtypes.float8_e5m2, 14)}[fmt]
    v = np.moveaxis(np.asarray(x, np.float32).astype(ml_dtypes.bfloat16).astype(np.float64), axis, -1)
    blocks = v.reshape(v.shape[:-1] + (-1, 32))
    amax = np.abs(blocks).max(-1, keepdims=True)
    byte = np.maximum(np.where(amax > 0, np.frexp(amax)[1] - 1 + 127, 0) - down, 1)
    scale = np.exp2(byte - 127.0)
    codes = (blocks / scale).astype(np.float32).astype(dtype).astype(np.float64)
    return np.moveaxis((codes * scale).reshape(v.shape), -1, axis)


WIDE = False


def mx_kscale(k):
    if not WIDE:
        return np.ones(k)
    levels = np.array([10, -10, 5, -5, 0])
    a = np.random.permutation(np.resize(levels, k // 512 * 4)).reshape(k // 512, 4)
    idx = np.arange(k)
    return np.exp2(a[idx // 512, idx % 128 // 32])


BF16 = ml_dtypes.bfloat16


def bf(x):
    return np.asarray(x, np.float32).astype(BF16)


def f64(x):
    return np.asarray(x).astype(np.float64)


N, IN, HID, OUT, NB = 2048, 512, 1024, 256, 64
EPS = 1e-8


def draw_adj():
    r = np.exp(0.5 * np.random.standard_normal(N))
    u = np.random.uniform(size=(N, N)) * (np.random.uniform(size=(N, N)) < NB / N)
    return u * r[:, None] * r[None, :]


def setup_inputs():
    t = mx_kscale(HID)
    return {"h": bf(np.maximum(np.random.standard_normal((N, HID)) * 0.9, 0.0) * t[None, :]),
            "adj": bf(draw_adj()),
            "W2": bf(np.random.standard_normal((OUT, HID)) * 2.0 / np.sqrt(HID) / t[None, :]),
            "b2": bf(np.random.standard_normal(OUT) * 0.3)}


def reference(h, adj, W2, b2):
    a = f64(adj)
    deg = a.sum(axis=1)
    d = 1.0 / np.sqrt(deg + EPS)
    norm_adj = d[:, None] * a * d[None, :]
    agg = mxq(norm_adj, 1, "e4m3") @ mxq(f64(h), 0, "e4m3")
    return (mxq(agg, 1, "e4m3") @ mxq(f64(W2), 1, "e4m3").T) + f64(b2)

@@ -1,0 +1,287 @@
+from contextlib import ExitStack
+
+import concourse.mybir as mybir
+from concourse.masks import make_identity
+
+F32 = mybir.dt.float32
+BF16 = mybir.dt.bfloat16
+U32 = mybir.dt.uint32
+U8 = mybir.dt.uint8
+FP8X4 = mybir.dt.float8_e4m3fn_x4
+ALU = mybir.AluOpType
+
+P = 128
+PACK = 4
+K_PASS = P * PACK
+
+NODES = 2048
+HID = 1024
+OUT = 256
+EPS = 1e-8
+
+ROW_TILES = NODES // P
+CHUNKS = NODES // K_PASS
+BANDS = CHUNKS
+TILES_PER_BAND = ROW_TILES // BANDS
+F_PASSES = HID // K_PASS
+EARLY_H_CHUNKS = 2
+
+FLOPS = 2 * NODES * NODES * HID + 2 * NODES * HID * OUT
+
+
+def tile_simplegcn_pb_kernel(tc, h, adj, W2, b2, out):
+    nc = tc.nc
+    with ExitStack() as stack:
+        keep = stack.enter_context(tc.tile_pool(name="keep", bufs=1))
+        small = stack.enter_context(tc.tile_pool(name="small", bufs=2))
+        h_stage = stack.enter_context(tc.tile_pool(name="h_stage", bufs=2))
+        a_stage = stack.enter_context(tc.tile_pool(name="a_stage", bufs=3))
+        g_stage = stack.enter_context(tc.tile_pool(name="g_stage", bufs=3))
+        o_stage = stack.enter_context(tc.tile_pool(name="o_stage", bufs=4))
+        turn_psum = stack.enter_context(tc.psum_pool(name="turn_psum", bufs=2))
+        agg_psum = stack.enter_context(tc.psum_pool(name="agg_psum", bufs=4))
+        out_psum = stack.enter_context(tc.psum_pool(name="out_psum", bufs=2))
+        stack.enter_context(tc.manual_schedule())
+
+        ident_f32 = keep.tile([P, P], F32)
+        ident_bf16 = keep.tile([P, P], BF16)
+        w2_rows = keep.tile([P, OUT // P, HID], BF16)
+        h_rows = keep.tile([P, CHUNKS, PACK, HID], BF16)
+        adj_rows = keep.tile([P, ROW_TILES, NODES], BF16)
+        bias_rows = keep.tile([P, OUT], BF16)
+        deg = keep.tile([P, ROW_TILES, 8], F32)
+        d_col = keep.tile([P, ROW_TILES], F32)
+        d_row = keep.tile([P, NODES], F32)
+        unused_scalar = keep.tile([P, NODES], BF16)
+        unused_vector = keep.tile([P, NODES], BF16)
+        h_codes = keep.tile([P, CHUNKS, HID], U32, align_bytes=64)
+        h_scales = keep.tile([P, CHUNKS, HID], U8, align_bytes=64)
+        w2_grouped = keep.tile([P, F_PASSES, OUT, PACK], BF16, align_bytes=64)
+        w2_codes = keep.tile([P, F_PASSES, OUT], U32, align_bytes=64)
+        w2_scales = keep.tile([P, F_PASSES, OUT], U8, align_bytes=64)
+
+        make_identity(nc, ident_f32[:])
+        make_identity(nc, ident_bf16[:])
+
+        def load_h(c):
+            nc.sync.dma_start(
+                out=h_rows[:, c, :, :].rearrange("p (u e) f -> p u (e f)", u=2),
+                in_=h[c * K_PASS : (c + 1) * K_PASS, :].rearrange("(u p e) f -> p u (e f)", u=2, e=2),
+            )
+
+        nc.sync.dma_start(out=w2_rows[:], in_=W2.rearrange("(b p) f -> p b f", p=P))
+        for c in range(EARLY_H_CHUNKS):
+            load_h(c)
+        for r in range(ROW_TILES):
+            nc.sync.dma_start(out=adj_rows[:, r, :], in_=adj[r * P : (r + 1) * P, :])
+        for c in range(EARLY_H_CHUNKS, CHUNKS):
+            load_h(c)
+        nc.sync.dma_start(out=bias_rows[:], in_=b2.partition_broadcast(P))
+
+        for g in range(F_PASSES):
+            for b in range(OUT // P):
+                w2_turned = turn_psum.tile([P, PACK, P], BF16, tag="turn")
+                for t in range(PACK):
+                    f0 = g * K_PASS + t * P
+                    nc.tensor.transpose(w2_turned[:, t, :], w2_rows[:, b, f0 : f0 + P], ident_bf16[:])
+                nc.scalar.copy(
+                    out=w2_grouped[:, g, b * P : (b + 1) * P, :],
+                    in_=w2_turned[:].rearrange("p t o -> p o t"),
+                )
+        nc.vector.quantize_mx(
+            out=w2_codes[:].rearrange("p g o -> p (g o)").bitcast(FP8X4),
+            scales=w2_scales[:].rearrange("p g o -> p (g o)"),
+            in_=w2_grouped[:].rearrange("p g o t -> p (g o t)"),
+        )
+
+        def quantise_h(c):
+            for g in range(F_PASSES):
+                cols = slice(g * K_PASS, (g + 1) * K_PASS)
+                h_grouped = h_stage.tile([P, K_PASS, PACK], BF16, align_bytes=64)
+                side_by_side = h_grouped[:].rearrange("p (a i) t -> p a t i", i=4)
+                row_by_row = h_rows[:, c, :, cols].rearrange("p t (a i) -> p a t i", i=4)
+                if g == 0:
+                    nc.vector.tensor_copy(out=side_by_side, in_=row_by_row)
+                else:
+                    nc.scalar.copy(out=side_by_side, in_=row_by_row)
+                nc.vector.quantize_mx(
+                    out=h_codes[:, c, cols].bitcast(FP8X4),
+                    scales=h_scales[:, c, cols],
+                    in_=h_grouped[:].rearrange("p f t -> p (f t)"),
+                )
+
+        for c in range(EARLY_H_CHUNKS):
+            quantise_h(c)
+
+        def sum_rows(r):
+            if r % 3 == 1:
+                nc.scalar.activation(
+                    out=unused_scalar[:],
+                    in_=adj_rows[:, r, :],
+                    func=mybir.ActivationFunctionType.Copy,
+                    accum_out=deg[:, r, 0:1],
+                )
+            else:
+                nc.vector.tensor_scalar(
+                    out=unused_vector[:],
+                    in0=adj_rows[:, r, :],
+                    scalar1=1.0,
+                    scalar2=None,
+                    op0=ALU.mult,
+                    op1=ALU.add,
+                    accum_out=deg[:, r, 0:1],
+                )
+
+        spread_banks = {}
+
+        def inverse_roots(band):
+            tiles = slice(band * TILES_PER_BAND, (band + 1) * TILES_PER_BAND)
+            x = small.tile([P, TILES_PER_BAND], F32)
+            root = small.tile([P, TILES_PER_BAND], F32)
+            y = small.tile([P, TILES_PER_BAND], F32)
+            half_xy = small.tile([P, TILES_PER_BAND], F32)
+            half_xyy = small.tile([P, TILES_PER_BAND], F32)
+            nc.vector.tensor_scalar_add(out=x[:], in0=deg[:, tiles, 0], scalar1=EPS)
+            nc.scalar.sqrt(out=root[:], in_=x[:])
+            nc.vector.reciprocal(out=y[:], in_=root[:])
+            nc.vector.scalar_tensor_tensor(
+                out=half_xy[:], in0=x[:], scalar=-0.5, in1=y[:], op0=ALU.mult, op1=ALU.mult
+            )
+            nc.vector.tensor_mul(out=half_xyy[:], in0=half_xy[:], in1=y[:])
+            nc.vector.scalar_tensor_tensor(
+                out=d_col[:, tiles], in0=half_xyy[:], scalar=1.5, in1=y[:], op0=ALU.add, op1=ALU.mult
+            )
+            spread = turn_psum.tile([P, TILES_PER_BAND, P], F32, tag="turn")
+            for k in range(TILES_PER_BAND):
+                r = band * TILES_PER_BAND + k
+                nc.tensor.matmul(
+                    out=spread[:, k, :],
+                    lhsT=d_col[:, r : r + 1].to_broadcast([P, P]),
+                    rhs=ident_f32[:],
+                    start=True,
+                    stop=True,
+                )
+            spread_banks[band] = spread
+
+        def keep_row(band):
+            nc.scalar.copy(
+                out=d_row[:, band * K_PASS : (band + 1) * K_PASS],
+                in_=spread_banks[band][:].rearrange("p k n -> p (k n)"),
+            )
+
+        for band in range(BANDS):
+            for k in range(TILES_PER_BAND):
+                sum_rows(band * TILES_PER_BAND + k)
+                if k == 1 and band > 0:
+                    keep_row(band - 1)
+            inverse_roots(band)
+        quantise_h(EARLY_H_CHUNKS)
+        keep_row(BANDS - 1)
+        for c in range(EARLY_H_CHUNKS + 1, CHUNKS):
+            quantise_h(c)
+
+        a_values = {}
+        a_operands = {}
+        g_values = {}
+        g_operands = {}
+        out_banks = {}
+
+        def normalise(r):
+            nc.vector.scalar_tensor_tensor(
+                out=adj_rows[:, r, :],
+                in0=adj_rows[:, r, :],
+                scalar=d_col[:, r : r + 1],
+                in1=d_row[:],
+                op0=ALU.mult,
+                op1=ALU.mult,
+            )
+
+        def turn(r):
+            words = adj_rows[:, r, :].bitcast(F32)
+            grouped = a_stage.tile([P, CHUNKS * K_PASS], BF16, align_bytes=64)
+            a_codes = a_stage.tile([P, CHUNKS, P], U32, align_bytes=64)
+            a_scales = a_stage.tile([P, CHUNKS, P], U8, align_bytes=64)
+            a_values[r] = grouped
+            a_operands[r] = (a_codes, a_scales)
+            grouped_words = grouped[:].bitcast(F32).rearrange("p (c i u) -> p c i u", c=CHUNKS, u=2)
+            for c0 in range(0, CHUNKS, 2):
+                turned = turn_psum.tile([P, 2, 2, P], F32, tag="turn")
+                for c in range(c0, c0 + 2):
+                    for u in range(2):
+                        w0 = c * (K_PASS // 2) + u * P
+                        nc.tensor.transpose(turned[:, c - c0, u, :], words[:, w0 : w0 + P], ident_f32[:])
+                nc.scalar.copy(
+                    out=grouped_words[:, c0 : c0 + 2, :, :], in_=turned[:].rearrange("p c u i -> p c i u")
+                )
+
+        def quantise_rows(r):
+            a_codes, a_scales = a_operands[r]
+            nc.vector.quantize_mx(
+                out=a_codes[:].rearrange("p c i -> p (c i)").bitcast(FP8X4),
+                scales=a_scales[:].rearrange("p c i -> p (c i)"),
+                in_=a_values[r][:],
+            )
+
+        def aggregate(r):
+            a_codes, a_scales = a_operands[r]
+            agg_grouped = g_stage.tile([P, F_PASSES, P, PACK], BF16, align_bytes=64)
+            agg_codes = g_stage.tile([P, F_PASSES, P], U32, align_bytes=64)
+            agg_scales = g_stage.tile([P, F_PASSES, P], U8, align_bytes=64)
+            g_values[r] = agg_grouped
+            g_operands[r] = (agg_codes, agg_scales)
+            for g in range(F_PASSES):
+                agg_t = agg_psum.tile([P, PACK, P], F32)
+                for t in range(PACK):
+                    f0 = g * K_PASS + t * P
+                    for c in range(CHUNKS):
+                        nc.tensor.matmul_mx(
+                            out=agg_t[:, t, :],
+                            lhsT=h_codes[:, c, f0 : f0 + P].bitcast(FP8X4),
+                            lhsT_scale=h_scales[:, c, f0 : f0 + P],
+                            rhs=a_codes[:, c, :].bitcast(FP8X4),
+                            rhs_scale=a_scales[:, c, :],
+                            start=(c == 0),
+                            stop=(c == CHUNKS - 1),
+                        )
+                nc.scalar.copy(out=agg_grouped[:, g, :, :], in_=agg_t[:].rearrange("p t i -> p i t"))
+
+        def quantise_agg(r):
+            agg_codes, agg_scales = g_operands[r]
+            nc.vector.quantize_mx(
+                out=agg_codes[:].rearrange("p g i -> p (g i)").bitcast(FP8X4),
+                scales=agg_scales[:].rearrange("p g i -> p (g i)"),
+                in_=g_values[r][:].rearrange("p g i t -> p (g i t)"),
+            )
+
+        def project(r):
+            agg_codes, agg_scales = g_operands[r]
+            out_rows = out_psum.tile([P, OUT], F32)
+            out_banks[r] = out_rows
+            for g in range(F_PASSES):
+                nc.tensor.matmul_mx(
+                    out=out_rows[:],
+                    lhsT=agg_codes[:, g, :].bitcast(FP8X4),
+                    lhsT_scale=agg_scales[:, g, :],
+                    rhs=w2_codes[:, g, :].bitcast(FP8X4),
+                    rhs_scale=w2_scales[:, g, :],
+                    start=(g == 0),
+                    stop=(g == F_PASSES - 1),
+                )
+
+        def finish(r):
+            result = o_stage.tile([P, OUT], F32)
+            nc.vector.tensor_tensor(out=result[:], in0=out_banks[r][:], in1=bias_rows[:], op=ALU.add)
+            nc.sync.dma_start(out=out[r * P : (r + 1) * P, :], in_=result[:])
+
+        def staged(stage, r):
+            if 0 <= r < ROW_TILES:
+                stage(r)
+
+        for k in range(-3, ROW_TILES + 2):
+            staged(finish, k - 2)
+            staged(quantise_agg, k - 1)
+            staged(quantise_rows, k + 1)
+            staged(normalise, k + 3)
+            staged(aggregate, k)
+            staged(project, k - 1)
+            staged(turn, k + 2)

@@ -24,7 +24,7 @@ CHUNKS = NODES // K_PASS
 BANDS = CHUNKS
 TILES_PER_BAND = ROW_TILES // BANDS
 F_PASSES = HID // K_PASS
-EARLY_H_CHUNKS = 2
+EARLY_H_CHUNKS = 1
 
 FLOPS = 2 * NODES * NODES * HID + 2 * NODES * HID * OUT
 
@@ -50,16 +50,17 @@ def tile_simplegcn_pb_kernel(tc, h, adj, W2, b2, out):
         adj_rows = keep.tile([P, ROW_TILES, NODES], BF16)
         bias_rows = keep.tile([P, OUT], BF16)
         deg = keep.tile([P, ROW_TILES, 8], F32)
+        eps_col = keep.tile([P, 1], F32)
         d_col = keep.tile([P, ROW_TILES], F32)
         d_row = keep.tile([P, NODES], F32)
         unused_scalar = keep.tile([P, NODES], BF16)
-        unused_vector = keep.tile([P, NODES], BF16)
         h_codes = keep.tile([P, CHUNKS, HID], U32, align_bytes=64)
         h_scales = keep.tile([P, CHUNKS, HID], U8, align_bytes=64)
         w2_grouped = keep.tile([P, F_PASSES, OUT, PACK], BF16, align_bytes=64)
         w2_codes = keep.tile([P, F_PASSES, OUT], U32, align_bytes=64)
         w2_scales = keep.tile([P, F_PASSES, OUT], U8, align_bytes=64)
 
+        nc.gpsimd.memset(eps_col[:], EPS)
         make_identity(nc, ident_f32[:])
         make_identity(nc, ident_bf16[:])
 
@@ -114,7 +115,7 @@ def tile_simplegcn_pb_kernel(tc, h, adj, W2, b2, out):
             quantise_h(c)
 
         def sum_rows(r):
-            if r % 3 == 1:
+            if r % TILES_PER_BAND == 0:
                 nc.scalar.activation(
                     out=unused_scalar[:],
                     in_=adj_rows[:, r, :],
@@ -122,6 +123,7 @@ def tile_simplegcn_pb_kernel(tc, h, adj, W2, b2, out):
                     accum_out=deg[:, r, 0:1],
                 )
             else:
+                unused_vector = small.tile([P, NODES], BF16)
                 nc.vector.tensor_scalar(
                     out=unused_vector[:],
                     in0=adj_rows[:, r, :],
@@ -136,21 +138,14 @@ def tile_simplegcn_pb_kernel(tc, h, adj, W2, b2, out):
 
         def inverse_roots(band):
             tiles = slice(band * TILES_PER_BAND, (band + 1) * TILES_PER_BAND)
-            x = small.tile([P, TILES_PER_BAND], F32)
             root = small.tile([P, TILES_PER_BAND], F32)
-            y = small.tile([P, TILES_PER_BAND], F32)
-            half_xy = small.tile([P, TILES_PER_BAND], F32)
-            half_xyy = small.tile([P, TILES_PER_BAND], F32)
-            nc.vector.tensor_scalar_add(out=x[:], in0=deg[:, tiles, 0], scalar1=EPS)
-            nc.scalar.sqrt(out=root[:], in_=x[:])
-            nc.vector.reciprocal(out=y[:], in_=root[:])
-            nc.vector.scalar_tensor_tensor(
-                out=half_xy[:], in0=x[:], scalar=-0.5, in1=y[:], op0=ALU.mult, op1=ALU.mult
+            nc.scalar.activation(
+                out=root[:],
+                in_=deg[:, tiles, 0],
+                func=mybir.ActivationFunctionType.Sqrt,
+                bias=eps_col[:],
             )
-            nc.vector.tensor_mul(out=half_xyy[:], in0=half_xy[:], in1=y[:])
-            nc.vector.scalar_tensor_tensor(
-                out=d_col[:, tiles], in0=half_xyy[:], scalar=1.5, in1=y[:], op0=ALU.add, op1=ALU.mult
-            )
+            nc.vector.reciprocal(out=d_col[:, tiles], in_=root[:])
             spread = turn_psum.tile([P, TILES_PER_BAND, P], F32, tag="turn")
             for k in range(TILES_PER_BAND):
                 r = band * TILES_PER_BAND + k
@@ -177,8 +172,6 @@ def tile_simplegcn_pb_kernel(tc, h, adj, W2, b2, out):
             inverse_roots(band)
         quantise_h(EARLY_H_CHUNKS)
         keep_row(BANDS - 1)
-        for c in range(EARLY_H_CHUNKS + 1, CHUNKS):
-            quantise_h(c)
 
         a_values = {}
         a_operands = {}
@@ -277,7 +270,10 @@ def tile_simplegcn_pb_kernel(tc, h, adj, W2, b2, out):
             if 0 <= r < ROW_TILES:
                 stage(r)
 
-        for k in range(-3, ROW_TILES + 2):
+        normalise(0)
+        for c in range(EARLY_H_CHUNKS + 1, CHUNKS):
+            quantise_h(c)
+        for k in range(-2, ROW_TILES + 2):
             staged(finish, k - 2)
             staged(quantise_agg, k - 1)
             staged(quantise_rows, k + 1)

@@ -9,6 +9,7 @@ U32 = mybir.dt.uint32
 U8 = mybir.dt.uint8
 FP8X4 = mybir.dt.float8_e4m3fn_x4
 ALU = mybir.AluOpType
+ACT = mybir.ActivationFunctionType
 
 P = 128
 PACK = 4
@@ -24,7 +25,9 @@ CHUNKS = NODES // K_PASS
 BANDS = CHUNKS
 TILES_PER_BAND = ROW_TILES // BANDS
 F_PASSES = HID // K_PASS
-EARLY_H_CHUNKS = 1
+O_TILES = OUT // P
+EARLY_TILES = TILES_PER_BAND
+PIECE_LAG = TILES_PER_BAND + 4
 
 FLOPS = 2 * NODES * NODES * HID + 2 * NODES * HID * OUT
 
@@ -34,7 +37,7 @@ def tile_simplegcn_pb_kernel(tc, h, adj, W2, b2, out):
     with ExitStack() as stack:
         keep = stack.enter_context(tc.tile_pool(name="keep", bufs=1))
         small = stack.enter_context(tc.tile_pool(name="small", bufs=2))
-        h_stage = stack.enter_context(tc.tile_pool(name="h_stage", bufs=2))
+        h_stage = stack.enter_context(tc.tile_pool(name="h_stage", bufs=3))
         a_stage = stack.enter_context(tc.tile_pool(name="a_stage", bufs=3))
         g_stage = stack.enter_context(tc.tile_pool(name="g_stage", bufs=3))
         o_stage = stack.enter_context(tc.tile_pool(name="o_stage", bufs=4))
@@ -45,7 +48,7 @@ def tile_simplegcn_pb_kernel(tc, h, adj, W2, b2, out):
 
         ident_f32 = keep.tile([P, P], F32)
         ident_bf16 = keep.tile([P, P], BF16)
-        w2_rows = keep.tile([P, OUT // P, HID], BF16)
+        w2_rows = keep.tile([P, O_TILES, HID], BF16)
         h_rows = keep.tile([P, CHUNKS, PACK, HID], BF16)
         adj_rows = keep.tile([P, ROW_TILES, NODES], BF16)
         bias_rows = keep.tile([P, OUT], BF16)
@@ -70,57 +73,60 @@ def tile_simplegcn_pb_kernel(tc, h, adj, W2, b2, out):
                 in_=h[c * K_PASS : (c + 1) * K_PASS, :].rearrange("(u p e) f -> p u (e f)", u=2, e=2),
             )
 
-        nc.sync.dma_start(out=w2_rows[:], in_=W2.rearrange("(b p) f -> p b f", p=P))
-        for c in range(EARLY_H_CHUNKS):
-            load_h(c)
+        load_h(0)
         for r in range(ROW_TILES):
             nc.sync.dma_start(out=adj_rows[:, r, :], in_=adj[r * P : (r + 1) * P, :])
-        for c in range(EARLY_H_CHUNKS, CHUNKS):
+        for c in range(1, CHUNKS):
             load_h(c)
+        nc.sync.dma_start(out=w2_rows[:], in_=W2.rearrange("(b p) f -> p b f", p=P))
         nc.sync.dma_start(out=bias_rows[:], in_=b2.partition_broadcast(P))
 
-        for g in range(F_PASSES):
-            for b in range(OUT // P):
-                w2_turned = turn_psum.tile([P, PACK, P], BF16, tag="turn")
-                for t in range(PACK):
-                    f0 = g * K_PASS + t * P
-                    nc.tensor.transpose(w2_turned[:, t, :], w2_rows[:, b, f0 : f0 + P], ident_bf16[:])
-                nc.scalar.copy(
-                    out=w2_grouped[:, g, b * P : (b + 1) * P, :],
-                    in_=w2_turned[:].rearrange("p t o -> p o t"),
-                )
-        nc.vector.quantize_mx(
-            out=w2_codes[:].rearrange("p g o -> p (g o)").bitcast(FP8X4),
-            scales=w2_scales[:].rearrange("p g o -> p (g o)"),
-            in_=w2_grouped[:].rearrange("p g o t -> p (g o t)"),
-        )
-
-        def quantise_h(c):
+        def turn_w2():
             for g in range(F_PASSES):
-                cols = slice(g * K_PASS, (g + 1) * K_PASS)
-                h_grouped = h_stage.tile([P, K_PASS, PACK], BF16, align_bytes=64)
-                side_by_side = h_grouped[:].rearrange("p (a i) t -> p a t i", i=4)
-                row_by_row = h_rows[:, c, :, cols].rearrange("p t (a i) -> p a t i", i=4)
+                w2_turned = out_psum.tile([P, O_TILES, PACK, P], BF16, tag="out")
+                for b in range(O_TILES):
+                    for t in range(PACK):
+                        f0 = g * K_PASS + t * P
+                        nc.tensor.transpose(w2_turned[:, b, t, :], w2_rows[:, b, f0 : f0 + P], ident_bf16[:])
+                side_by_side = w2_grouped[:, g, :, :].rearrange("p (b o) t -> p b o t", b=O_TILES)
+                plane_by_plane = w2_turned[:].rearrange("p b t o -> p b o t")
                 if g == 0:
-                    nc.vector.tensor_copy(out=side_by_side, in_=row_by_row)
+                    nc.vector.tensor_copy(out=side_by_side, in_=plane_by_plane)
                 else:
-                    nc.scalar.copy(out=side_by_side, in_=row_by_row)
-                nc.vector.quantize_mx(
-                    out=h_codes[:, c, cols].bitcast(FP8X4),
-                    scales=h_scales[:, c, cols],
-                    in_=h_grouped[:].rearrange("p f t -> p (f t)"),
-                )
+                    nc.scalar.copy(out=side_by_side, in_=plane_by_plane)
 
-        for c in range(EARLY_H_CHUNKS):
-            quantise_h(c)
+        def quantise_w2():
+            nc.vector.quantize_mx(
+                out=w2_codes[:].rearrange("p g o -> p (g o)").bitcast(FP8X4),
+                scales=w2_scales[:].rearrange("p g o -> p (g o)"),
+                in_=w2_grouped[:].rearrange("p g o t -> p (g o t)"),
+            )
+
+        h_values = {}
+
+        def regroup_h(c, g):
+            cols = slice(g * K_PASS, (g + 1) * K_PASS)
+            h_grouped = h_stage.tile([P, K_PASS, PACK], BF16, align_bytes=64, tag="h_grouped_%d" % g)
+            h_values[(c, g)] = h_grouped
+            side_by_side = h_grouped[:].rearrange("p (a i) t -> p a t i", i=4)
+            row_by_row = h_rows[:, c, :, cols].rearrange("p t (a i) -> p a t i", i=4)
+            if g == 0:
+                nc.vector.tensor_copy(out=side_by_side, in_=row_by_row)
+            else:
+                nc.scalar.copy(out=side_by_side, in_=row_by_row)
+
+        def quantise_h(c, g):
+            cols = slice(g * K_PASS, (g + 1) * K_PASS)
+            nc.vector.quantize_mx(
+                out=h_codes[:, c, cols].bitcast(FP8X4),
+                scales=h_scales[:, c, cols],
+                in_=h_values[(c, g)][:].rearrange("p f t -> p (f t)"),
+            )
 
         def sum_rows(r):
             if r % TILES_PER_BAND == 0:
                 nc.scalar.activation(
-                    out=unused_scalar[:],
-                    in_=adj_rows[:, r, :],
-                    func=mybir.ActivationFunctionType.Copy,
-                    accum_out=deg[:, r, 0:1],
+                    out=unused_scalar[:], in_=adj_rows[:, r, :], func=ACT.Copy, accum_out=deg[:, r, 0:1]
                 )
             else:
                 unused_vector = small.tile([P, NODES], BF16)
@@ -134,19 +140,20 @@ def tile_simplegcn_pb_kernel(tc, h, adj, W2, b2, out):
                     accum_out=deg[:, r, 0:1],
                 )
 
+        roots = {}
         spread_banks = {}
 
-        def inverse_roots(band):
+        def take_roots(band):
             tiles = slice(band * TILES_PER_BAND, (band + 1) * TILES_PER_BAND)
             root = small.tile([P, TILES_PER_BAND], F32)
-            nc.scalar.activation(
-                out=root[:],
-                in_=deg[:, tiles, 0],
-                func=mybir.ActivationFunctionType.Sqrt,
-                bias=eps_col[:],
-            )
-            nc.vector.reciprocal(out=d_col[:, tiles], in_=root[:])
-            spread = turn_psum.tile([P, TILES_PER_BAND, P], F32, tag="turn")
+            roots[band] = root
+            nc.scalar.activation(out=root[:], in_=deg[:, tiles, 0], func=ACT.Sqrt, bias=eps_col[:])
+
+        def invert_and_spread(band):
+            tiles = slice(band * TILES_PER_BAND, (band + 1) * TILES_PER_BAND)
+            nc.vector.reciprocal(out=d_col[:, tiles], in_=roots[band][:])
+            spread = agg_psum.tile([P, TILES_PER_BAND, P], F32, tag="agg")
+            spread_banks[band] = spread
             for k in range(TILES_PER_BAND):
                 r = band * TILES_PER_BAND + k
                 nc.tensor.matmul(
@@ -156,7 +163,6 @@ def tile_simplegcn_pb_kernel(tc, h, adj, W2, b2, out):
                     start=True,
                     stop=True,
                 )
-            spread_banks[band] = spread
 
         def keep_row(band):
             nc.scalar.copy(
@@ -164,30 +170,35 @@ def tile_simplegcn_pb_kernel(tc, h, adj, W2, b2, out):
                 in_=spread_banks[band][:].rearrange("p k n -> p (k n)"),
             )
 
-        for band in range(BANDS):
-            for k in range(TILES_PER_BAND):
-                sum_rows(band * TILES_PER_BAND + k)
-                if k == 1 and band > 0:
-                    keep_row(band - 1)
-            inverse_roots(band)
-        quantise_h(EARLY_H_CHUNKS)
-        keep_row(BANDS - 1)
-
         a_values = {}
         a_operands = {}
         g_values = {}
         g_operands = {}
         out_banks = {}
 
-        def normalise(r):
+        def normalise_piece(r, c):
+            cols = slice(c * K_PASS, (c + 1) * K_PASS)
             nc.vector.scalar_tensor_tensor(
-                out=adj_rows[:, r, :],
-                in0=adj_rows[:, r, :],
+                out=adj_rows[:, r, cols],
+                in0=adj_rows[:, r, cols],
                 scalar=d_col[:, r : r + 1],
-                in1=d_row[:],
+                in1=d_row[:, cols],
                 op0=ALU.mult,
                 op1=ALU.mult,
             )
+
+        def normalise_rest(r):
+            if r < EARLY_TILES:
+                normalise_piece(r, CHUNKS - 1)
+            else:
+                nc.vector.scalar_tensor_tensor(
+                    out=adj_rows[:, r, :],
+                    in0=adj_rows[:, r, :],
+                    scalar=d_col[:, r : r + 1],
+                    in1=d_row[:],
+                    op0=ALU.mult,
+                    op1=ALU.mult,
+                )
 
         def turn(r):
             words = adj_rows[:, r, :].bitcast(F32)
@@ -223,7 +234,7 @@ def tile_simplegcn_pb_kernel(tc, h, adj, W2, b2, out):
             g_values[r] = agg_grouped
             g_operands[r] = (agg_codes, agg_scales)
             for g in range(F_PASSES):
-                agg_t = agg_psum.tile([P, PACK, P], F32)
+                agg_t = agg_psum.tile([P, PACK, P], F32, tag="agg")
                 for t in range(PACK):
                     f0 = g * K_PASS + t * P
                     for c in range(CHUNKS):
@@ -248,7 +259,7 @@ def tile_simplegcn_pb_kernel(tc, h, adj, W2, b2, out):
 
         def project(r):
             agg_codes, agg_scales = g_operands[r]
-            out_rows = out_psum.tile([P, OUT], F32)
+            out_rows = out_psum.tile([P, OUT], F32, tag="out")
             out_banks[r] = out_rows
             for g in range(F_PASSES):
                 nc.tensor.matmul_mx(
@@ -266,18 +277,53 @@ def tile_simplegcn_pb_kernel(tc, h, adj, W2, b2, out):
             nc.vector.tensor_tensor(out=result[:], in0=out_banks[r][:], in1=bias_rows[:], op=ALU.add)
             nc.sync.dma_start(out=out[r * P : (r + 1) * P, :], in_=result[:])
 
+        for g in range(F_PASSES):
+            regroup_h(0, g)
+        for g in range(F_PASSES):
+            quantise_h(0, g)
+        for s in range(PIECE_LAG + EARLY_TILES * (CHUNKS - 1)):
+            band, k = divmod(s, TILES_PER_BAND)
+            closes_band = band < BANDS and k == TILES_PER_BAND - 1
+            if band < BANDS:
+                sum_rows(s)
+            if closes_band:
+                take_roots(band)
+            c, r = divmod(s - PIECE_LAG, EARLY_TILES)
+            if c >= 0:
+                normalise_piece(r, c)
+            if closes_band:
+                invert_and_spread(band)
+            if 0 < band < BANDS and k == TILES_PER_BAND - 2:
+                keep_row(band - 1)
+
         def staged(stage, r):
             if 0 <= r < ROW_TILES:
                 stage(r)
 
-        normalise(0)
-        for c in range(EARLY_H_CHUNKS + 1, CHUNKS):
-            quantise_h(c)
+        regroup_h(1, 0)
+        regroup_h(1, 1)
+        quantise_h(1, 0)
+        keep_row(BANDS - 1)
+        regroup_h(2, 1)
+        normalise_rest(0)
         for k in range(-2, ROW_TILES + 2):
             staged(finish, k - 2)
             staged(quantise_agg, k - 1)
             staged(quantise_rows, k + 1)
-            staged(normalise, k + 3)
+            if k == -1:
+                for c in range(1, CHUNKS):
+                    quantise_h(c, 1)
+            staged(normalise_rest, k + 3)
             staged(aggregate, k)
             staged(project, k - 1)
             staged(turn, k + 2)
+            if k == -2:
+                regroup_h(2, 0)
+                regroup_h(3, 0)
+                regroup_h(3, 1)
+                quantise_h(2, 0)
+                quantise_h(3, 0)
+            if k == -1:
+                turn_w2()
+            if k == 0:
+                quantise_w2()

@@ -56,7 +56,6 @@ def tile_simplegcn_pb_kernel(tc, h, adj, W2, b2, out):
         eps_col = keep.tile([P, 1], F32)
         d_col = keep.tile([P, ROW_TILES], F32)
         d_row = keep.tile([P, NODES], F32)
-        unused_scalar = keep.tile([P, NODES], BF16)
         h_codes = keep.tile([P, CHUNKS, HID], U32, align_bytes=64)
         h_scales = keep.tile([P, CHUNKS, HID], U8, align_bytes=64)
         w2_grouped = keep.tile([P, F_PASSES, OUT, PACK], BF16, align_bytes=64)
@@ -124,7 +123,8 @@ def tile_simplegcn_pb_kernel(tc, h, adj, W2, b2, out):
             )
 
         def sum_rows(r):
-            if r % TILES_PER_BAND == 0:
+            if r % 2 == 0:
+                unused_scalar = small.tile([P, NODES], BF16)
                 nc.scalar.activation(
                     out=unused_scalar[:], in_=adj_rows[:, r, :], func=ACT.Copy, accum_out=deg[:, r, 0:1]
                 )
@@ -154,10 +154,10 @@ def tile_simplegcn_pb_kernel(tc, h, adj, W2, b2, out):
             nc.vector.reciprocal(out=d_col[:, tiles], in_=roots[band][:])
             spread = agg_psum.tile([P, TILES_PER_BAND, P], F32, tag="agg")
             spread_banks[band] = spread
-            for k in range(TILES_PER_BAND):
-                r = band * TILES_PER_BAND + k
+            for place in range(TILES_PER_BAND):
+                r = band * TILES_PER_BAND + place
                 nc.tensor.matmul(
-                    out=spread[:, k, :],
+                    out=spread[:, place, :],
                     lhsT=d_col[:, r : r + 1].to_broadcast([P, P]),
                     rhs=ident_f32[:],
                     start=True,
@@ -167,7 +167,7 @@ def tile_simplegcn_pb_kernel(tc, h, adj, W2, b2, out):
         def keep_row(band):
             nc.scalar.copy(
                 out=d_row[:, band * K_PASS : (band + 1) * K_PASS],
-                in_=spread_banks[band][:].rearrange("p k n -> p (k n)"),
+                in_=spread_banks[band][:].rearrange("p l n -> p (l n)"),
             )
 
         a_values = {}
@@ -282,8 +282,8 @@ def tile_simplegcn_pb_kernel(tc, h, adj, W2, b2, out):
         for g in range(F_PASSES):
             quantise_h(0, g)
         for s in range(PIECE_LAG + EARLY_TILES * (CHUNKS - 1)):
-            band, k = divmod(s, TILES_PER_BAND)
-            closes_band = band < BANDS and k == TILES_PER_BAND - 1
+            band, place = divmod(s, TILES_PER_BAND)
+            closes_band = band < BANDS and place == TILES_PER_BAND - 1
             if band < BANDS:
                 sum_rows(s)
             if closes_band:
@@ -293,7 +293,7 @@ def tile_simplegcn_pb_kernel(tc, h, adj, W2, b2, out):
                 normalise_piece(r, c)
             if closes_band:
                 invert_and_spread(band)
-            if 0 < band < BANDS and k == TILES_PER_BAND - 2:
+            if 0 < band < BANDS and place == TILES_PER_BAND - 2:
                 keep_row(band - 1)
 
         def staged(stage, r):

@@ -22,12 +22,9 @@ EPS = 1e-8
 
 ROW_TILES = NODES // P
 CHUNKS = NODES // K_PASS
-BANDS = CHUNKS
-TILES_PER_BAND = ROW_TILES // BANDS
 F_PASSES = HID // K_PASS
 O_TILES = OUT // P
-EARLY_TILES = TILES_PER_BAND
-PIECE_LAG = TILES_PER_BAND + 4
+SUM_WIDTH = 256
 
 FLOPS = 2 * NODES * NODES * HID + 2 * NODES * HID * OUT
 
@@ -37,8 +34,9 @@ def tile_simplegcn_pb_kernel(tc, h, adj, W2, b2, out):
     with ExitStack() as stack:
         keep = stack.enter_context(tc.tile_pool(name="keep", bufs=1))
         small = stack.enter_context(tc.tile_pool(name="small", bufs=2))
-        h_stage = stack.enter_context(tc.tile_pool(name="h_stage", bufs=3))
-        a_stage = stack.enter_context(tc.tile_pool(name="a_stage", bufs=3))
+        h_stage = stack.enter_context(tc.tile_pool(name="h_stage", bufs=5))
+        u_stage = stack.enter_context(tc.tile_pool(name="u_stage", bufs=4))
+        a_stage = stack.enter_context(tc.tile_pool(name="a_stage", bufs=4))
         g_stage = stack.enter_context(tc.tile_pool(name="g_stage", bufs=3))
         o_stage = stack.enter_context(tc.tile_pool(name="o_stage", bufs=4))
         turn_psum = stack.enter_context(tc.psum_pool(name="turn_psum", bufs=2))
@@ -49,7 +47,9 @@ def tile_simplegcn_pb_kernel(tc, h, adj, W2, b2, out):
         ident_f32 = keep.tile([P, P], F32)
         ident_bf16 = keep.tile([P, P], BF16)
         w2_rows = keep.tile([P, O_TILES, HID], BF16)
-        h_rows = keep.tile([P, CHUNKS, PACK, HID], BF16)
+        h_rows_0 = keep.tile([P, CHUNKS, PACK, K_PASS], BF16)
+        h_rows_1 = keep.tile([P, CHUNKS, PACK, K_PASS], BF16)
+        h_rows = (h_rows_0, h_rows_1)
         adj_rows = keep.tile([P, ROW_TILES, NODES], BF16)
         bias_rows = keep.tile([P, OUT], BF16)
         deg = keep.tile([P, ROW_TILES, 8], F32)
@@ -63,36 +63,42 @@ def tile_simplegcn_pb_kernel(tc, h, adj, W2, b2, out):
         w2_scales = keep.tile([P, F_PASSES, OUT], U8, align_bytes=64)
 
         nc.gpsimd.memset(eps_col[:], EPS)
-        make_identity(nc, ident_f32[:])
         make_identity(nc, ident_bf16[:])
+        make_identity(nc, ident_f32[:])
 
-        def load_h(c):
-            nc.sync.dma_start(
-                out=h_rows[:, c, :, :].rearrange("p (u e) f -> p u (e f)", u=2),
-                in_=h[c * K_PASS : (c + 1) * K_PASS, :].rearrange("(u p e) f -> p u (e f)", u=2, e=2),
-            )
+        def load_h(c, g):
+            cols = slice(g * K_PASS, (g + 1) * K_PASS)
+            for u in range(2):
+                j0 = c * K_PASS + u * (K_PASS // 2)
+                nc.sync.dma_start(
+                    out=h_rows[g][:, c, 2 * u : 2 * u + 2, :],
+                    in_=h[j0 : j0 + K_PASS // 2, cols].rearrange("(p e) f -> p e f", e=2),
+                )
 
-        load_h(0)
-        for r in range(ROW_TILES):
+        load_h(0, 0)
+        load_h(1, 0)
+        load_h(2, 0)
+        load_h(3, 0)
+        for r in range(ROW_TILES - 1):
             nc.sync.dma_start(out=adj_rows[:, r, :], in_=adj[r * P : (r + 1) * P, :])
-        for c in range(1, CHUNKS):
-            load_h(c)
+        for half in range(2):
+            cols = slice(half * NODES // 2, (half + 1) * NODES // 2)
+            nc.sync.dma_start(out=adj_rows[:, ROW_TILES - 1, cols], in_=adj[NODES - P :, cols])
+        for c in range(CHUNKS):
+            load_h(c, 1)
         nc.sync.dma_start(out=w2_rows[:], in_=W2.rearrange("(b p) f -> p b f", p=P))
         nc.sync.dma_start(out=bias_rows[:], in_=b2.partition_broadcast(P))
 
-        def turn_w2():
-            for g in range(F_PASSES):
-                w2_turned = out_psum.tile([P, O_TILES, PACK, P], BF16, tag="out")
-                for b in range(O_TILES):
-                    for t in range(PACK):
-                        f0 = g * K_PASS + t * P
-                        nc.tensor.transpose(w2_turned[:, b, t, :], w2_rows[:, b, f0 : f0 + P], ident_bf16[:])
-                side_by_side = w2_grouped[:, g, :, :].rearrange("p (b o) t -> p b o t", b=O_TILES)
-                plane_by_plane = w2_turned[:].rearrange("p b t o -> p b o t")
-                if g == 0:
-                    nc.vector.tensor_copy(out=side_by_side, in_=plane_by_plane)
-                else:
-                    nc.scalar.copy(out=side_by_side, in_=plane_by_plane)
+        def turn_w2(g):
+            w2_turned = out_psum.tile([P, O_TILES, PACK, P], BF16, tag="out")
+            for b in range(O_TILES):
+                for t in range(PACK):
+                    f0 = g * K_PASS + t * P
+                    nc.tensor.transpose(w2_turned[:, b, t, :], w2_rows[:, b, f0 : f0 + P], ident_bf16[:])
+            nc.scalar.copy(
+                out=w2_grouped[:, g, :, :].rearrange("p (b o) t -> p b o t", b=O_TILES),
+                in_=w2_turned[:].rearrange("p b t o -> p b o t"),
+            )
 
         def quantise_w2():
             nc.vector.quantize_mx(
@@ -103,16 +109,16 @@ def tile_simplegcn_pb_kernel(tc, h, adj, W2, b2, out):
 
         h_values = {}
 
-        def regroup_h(c, g):
-            cols = slice(g * K_PASS, (g + 1) * K_PASS)
-            h_grouped = h_stage.tile([P, K_PASS, PACK], BF16, align_bytes=64, tag="h_grouped_%d" % g)
+        def gcopy(out, in_):
+            nc.gpsimd.tensor_scalar(out=out, in0=in_, scalar1=1.0, scalar2=0.0, op0=ALU.mult, op1=ALU.add)
+
+        def regroup_h(c, g, copy):
+            h_grouped = h_stage.tile([P, K_PASS, PACK], BF16, align_bytes=64)
             h_values[(c, g)] = h_grouped
-            side_by_side = h_grouped[:].rearrange("p (a i) t -> p a t i", i=4)
-            row_by_row = h_rows[:, c, :, cols].rearrange("p t (a i) -> p a t i", i=4)
-            if g == 0:
-                nc.vector.tensor_copy(out=side_by_side, in_=row_by_row)
-            else:
-                nc.scalar.copy(out=side_by_side, in_=row_by_row)
+            copy(
+                out=h_grouped[:].rearrange("p (a i) t -> p a t i", i=4),
+                in_=h_rows[g][:, c, :, :].rearrange("p t (a i) -> p a t i", i=4),
+            )
 
         def quantise_h(c, g):
             cols = slice(g * K_PASS, (g + 1) * K_PASS)
@@ -122,13 +128,8 @@ def tile_simplegcn_pb_kernel(tc, h, adj, W2, b2, out):
                 in_=h_values[(c, g)][:].rearrange("p f t -> p (f t)"),
             )
 
-        def sum_rows(r):
-            if r % 2 == 0:
-                unused_scalar = small.tile([P, NODES], BF16)
-                nc.scalar.activation(
-                    out=unused_scalar[:], in_=adj_rows[:, r, :], func=ACT.Copy, accum_out=deg[:, r, 0:1]
-                )
-            else:
+        def sum_direct(r, on_vector):
+            if on_vector:
                 unused_vector = small.tile([P, NODES], BF16)
                 nc.vector.tensor_scalar(
                     out=unused_vector[:],
@@ -139,107 +140,100 @@ def tile_simplegcn_pb_kernel(tc, h, adj, W2, b2, out):
                     op1=ALU.add,
                     accum_out=deg[:, r, 0:1],
                 )
-
-        roots = {}
-        spread_banks = {}
-
-        def take_roots(band):
-            tiles = slice(band * TILES_PER_BAND, (band + 1) * TILES_PER_BAND)
-            root = small.tile([P, TILES_PER_BAND], F32)
-            roots[band] = root
-            nc.scalar.activation(out=root[:], in_=deg[:, tiles, 0], func=ACT.Sqrt, bias=eps_col[:])
-
-        def invert_and_spread(band):
-            tiles = slice(band * TILES_PER_BAND, (band + 1) * TILES_PER_BAND)
-            nc.vector.reciprocal(out=d_col[:, tiles], in_=roots[band][:])
-            spread = agg_psum.tile([P, TILES_PER_BAND, P], F32, tag="agg")
-            spread_banks[band] = spread
-            for place in range(TILES_PER_BAND):
-                r = band * TILES_PER_BAND + place
-                nc.tensor.matmul(
-                    out=spread[:, place, :],
-                    lhsT=d_col[:, r : r + 1].to_broadcast([P, P]),
-                    rhs=ident_f32[:],
-                    start=True,
-                    stop=True,
+            else:
+                unused_scalar = small.tile([P, NODES], BF16)
+                nc.scalar.activation(
+                    out=unused_scalar[:], in_=adj_rows[:, r, :], func=ACT.Copy, accum_out=deg[:, r, 0:1]
                 )
 
-        def keep_row(band):
+        def sum_folded(r):
+            folded = agg_psum.tile([P, SUM_WIDTH], F32, tag="agg")
+            for n in range(NODES // SUM_WIDTH):
+                nc.tensor.matmul(
+                    out=folded[:],
+                    lhsT=ident_bf16[:],
+                    rhs=adj_rows[:, r, n * SUM_WIDTH : (n + 1) * SUM_WIDTH],
+                    start=(n == 0),
+                    stop=(n == NODES // SUM_WIDTH - 1),
+                )
+            unused_folded = small.tile([P, SUM_WIDTH], BF16)
+            nc.scalar.activation(out=unused_folded[:], in_=folded[:], func=ACT.Copy, accum_out=deg[:, r, 0:1])
+
+        def invert(r0, n):
+            nc.scalar.activation(
+                out=d_col[:, r0 : r0 + n], in_=deg[:, r0 : r0 + n, 0], func=ACT.Abs_reciprocal_sqrt, bias=eps_col[:]
+            )
+
+        spread_banks = {}
+
+        def spread(r0, n):
+            bank = out_psum.tile([P, PACK, P], F32, tag="out")
+            for place in range(n):
+                r = r0 + place
+                nc.tensor.transpose(bank[:, place, :], d_col[:, r : r + 1].to_broadcast([P, P]), ident_f32[:])
+            spread_banks[r0] = bank
+
+        def keep_row(r0, n):
             nc.scalar.copy(
-                out=d_row[:, band * K_PASS : (band + 1) * K_PASS],
-                in_=spread_banks[band][:].rearrange("p l n -> p (l n)"),
+                out=d_row[:, r0 * P : (r0 + n) * P],
+                in_=spread_banks[r0][:, 0:n, :].rearrange("p l n -> p (l n)"),
             )
 
-        a_values = {}
-        a_operands = {}
-        g_values = {}
-        g_operands = {}
-        out_banks = {}
+        row_operands = {}
+        unit_values = {}
 
-        def normalise_piece(r, c):
+        def normalise(m, c):
             cols = slice(c * K_PASS, (c + 1) * K_PASS)
-            nc.vector.scalar_tensor_tensor(
-                out=adj_rows[:, r, cols],
-                in0=adj_rows[:, r, cols],
-                scalar=d_col[:, r : r + 1],
-                in1=d_row[:, cols],
-                op0=ALU.mult,
-                op1=ALU.mult,
-            )
-
-        def normalise_rest(r):
-            if r < EARLY_TILES:
-                normalise_piece(r, CHUNKS - 1)
-            else:
+            for r in (2 * m, 2 * m + 1):
                 nc.vector.scalar_tensor_tensor(
-                    out=adj_rows[:, r, :],
-                    in0=adj_rows[:, r, :],
+                    out=adj_rows[:, r, cols],
+                    in0=adj_rows[:, r, cols],
                     scalar=d_col[:, r : r + 1],
-                    in1=d_row[:],
+                    in1=d_row[:, cols],
                     op0=ALU.mult,
                     op1=ALU.mult,
                 )
 
-        def turn(r):
-            words = adj_rows[:, r, :].bitcast(F32)
-            grouped = a_stage.tile([P, CHUNKS * K_PASS], BF16, align_bytes=64)
-            a_codes = a_stage.tile([P, CHUNKS, P], U32, align_bytes=64)
-            a_scales = a_stage.tile([P, CHUNKS, P], U8, align_bytes=64)
-            a_values[r] = grouped
-            a_operands[r] = (a_codes, a_scales)
-            grouped_words = grouped[:].bitcast(F32).rearrange("p (c i u) -> p c i u", c=CHUNKS, u=2)
-            for c0 in range(0, CHUNKS, 2):
-                turned = turn_psum.tile([P, 2, 2, P], F32, tag="turn")
-                for c in range(c0, c0 + 2):
-                    for u in range(2):
-                        w0 = c * (K_PASS // 2) + u * P
-                        nc.tensor.transpose(turned[:, c - c0, u, :], words[:, w0 : w0 + P], ident_f32[:])
-                nc.scalar.copy(
-                    out=grouped_words[:, c0 : c0 + 2, :, :], in_=turned[:].rearrange("p c u i -> p c i u")
-                )
-
-        def quantise_rows(r):
-            a_codes, a_scales = a_operands[r]
-            nc.vector.quantize_mx(
-                out=a_codes[:].rearrange("p c i -> p (c i)").bitcast(FP8X4),
-                scales=a_scales[:].rearrange("p c i -> p (c i)"),
-                in_=a_values[r][:],
+        def turn(m, c):
+            turned = turn_psum.tile([P, 2, 2, P], F32, tag="turn")
+            grouped = u_stage.tile([P, 2 * K_PASS], BF16, align_bytes=64)
+            unit_values[(m, c)] = grouped
+            for place in range(2):
+                words = adj_rows[:, 2 * m + place, :].bitcast(F32)
+                for u in range(2):
+                    w0 = c * (K_PASS // 2) + u * P
+                    nc.tensor.transpose(turned[:, place, u, :], words[:, w0 : w0 + P], ident_f32[:])
+            nc.scalar.copy(
+                out=grouped[:].bitcast(F32).rearrange("p (l i u) -> p l i u", l=2, u=2),
+                in_=turned[:].rearrange("p l u i -> p l i u"),
             )
 
-        def aggregate(r):
-            a_codes, a_scales = a_operands[r]
-            agg_grouped = g_stage.tile([P, F_PASSES, P, PACK], BF16, align_bytes=64)
-            agg_codes = g_stage.tile([P, F_PASSES, P], U32, align_bytes=64)
-            agg_scales = g_stage.tile([P, F_PASSES, P], U8, align_bytes=64)
-            g_values[r] = agg_grouped
-            g_operands[r] = (agg_codes, agg_scales)
-            for g in range(F_PASSES):
-                agg_t = agg_psum.tile([P, PACK, P], F32, tag="agg")
-                for t in range(PACK):
-                    f0 = g * K_PASS + t * P
+        def quantise_unit(m, c):
+            if m not in row_operands:
+                a_codes = a_stage.tile([P, CHUNKS, 2 * P], U32, align_bytes=64)
+                a_scales = a_stage.tile([P, CHUNKS, 2 * P], U8, align_bytes=64)
+                row_operands[m] = (a_codes, a_scales)
+            a_codes, a_scales = row_operands[m]
+            nc.vector.quantize_mx(
+                out=a_codes[:, c, :].bitcast(FP8X4), scales=a_scales[:, c, :], in_=unit_values[(m, c)][:]
+            )
+
+        g_values = {}
+        g_operands = {}
+        out_banks = {}
+
+        def aggregate(m, g):
+            if m not in g_values:
+                agg_grouped = g_stage.tile([P, F_PASSES, 2 * P, PACK], BF16, align_bytes=64)
+                g_values[m] = agg_grouped
+            a_codes, a_scales = row_operands[m]
+            for q in range(2):
+                agg_t = agg_psum.tile([P, 2, 2 * P], F32, tag="agg")
+                for s in range(2):
+                    f0 = g * K_PASS + (2 * q + s) * P
                     for c in range(CHUNKS):
                         nc.tensor.matmul_mx(
-                            out=agg_t[:, t, :],
+                            out=agg_t[:, s, :],
                             lhsT=h_codes[:, c, f0 : f0 + P].bitcast(FP8X4),
                             lhsT_scale=h_scales[:, c, f0 : f0 + P],
                             rhs=a_codes[:, c, :].bitcast(FP8X4),
@@ -247,83 +241,121 @@ def tile_simplegcn_pb_kernel(tc, h, adj, W2, b2, out):
                             start=(c == 0),
                             stop=(c == CHUNKS - 1),
                         )
-                nc.scalar.copy(out=agg_grouped[:, g, :, :], in_=agg_t[:].rearrange("p t i -> p i t"))
+                nc.scalar.copy(out=g_values[m][:, g, :, 2 * q : 2 * q + 2], in_=agg_t[:].rearrange("p s i -> p i s"))
 
-        def quantise_agg(r):
-            agg_codes, agg_scales = g_operands[r]
+        def quantise_agg(m):
+            agg_codes = g_stage.tile([P, F_PASSES, 2 * P], U32, align_bytes=64)
+            agg_scales = g_stage.tile([P, F_PASSES, 2 * P], U8, align_bytes=64)
+            g_operands[m] = (agg_codes, agg_scales)
             nc.vector.quantize_mx(
                 out=agg_codes[:].rearrange("p g i -> p (g i)").bitcast(FP8X4),
                 scales=agg_scales[:].rearrange("p g i -> p (g i)"),
-                in_=g_values[r][:].rearrange("p g i t -> p (g i t)"),
+                in_=g_values[m][:].rearrange("p g i t -> p (g i t)"),
             )
 
-        def project(r):
-            agg_codes, agg_scales = g_operands[r]
-            out_rows = out_psum.tile([P, OUT], F32, tag="out")
-            out_banks[r] = out_rows
-            for g in range(F_PASSES):
-                nc.tensor.matmul_mx(
-                    out=out_rows[:],
-                    lhsT=agg_codes[:, g, :].bitcast(FP8X4),
-                    lhsT_scale=agg_scales[:, g, :],
-                    rhs=w2_codes[:, g, :].bitcast(FP8X4),
-                    rhs_scale=w2_scales[:, g, :],
-                    start=(g == 0),
-                    stop=(g == F_PASSES - 1),
-                )
+        def project(m):
+            agg_codes, agg_scales = g_operands[m]
+            out_rows = out_psum.tile([P, 2, OUT], F32, tag="out")
+            out_banks[m] = out_rows
+            for place in range(2):
+                cols = slice(place * P, (place + 1) * P)
+                for g in range(F_PASSES):
+                    nc.tensor.matmul_mx(
+                        out=out_rows[:, place, :],
+                        lhsT=agg_codes[:, g, cols].bitcast(FP8X4),
+                        lhsT_scale=agg_scales[:, g, cols],
+                        rhs=w2_codes[:, g, :].bitcast(FP8X4),
+                        rhs_scale=w2_scales[:, g, :],
+                        start=(g == 0),
+                        stop=(g == F_PASSES - 1),
+                    )
 
-        def finish(r):
-            result = o_stage.tile([P, OUT], F32)
-            nc.vector.tensor_tensor(out=result[:], in0=out_banks[r][:], in1=bias_rows[:], op=ALU.add)
-            nc.sync.dma_start(out=out[r * P : (r + 1) * P, :], in_=result[:])
+        def finish(m):
+            for place in range(2):
+                r = 2 * m + place
+                result = o_stage.tile([P, OUT], F32)
+                nc.vector.tensor_tensor(out=result[:], in0=out_banks[m][:, place, :], in1=bias_rows[:], op=ALU.add)
+                nc.sync.dma_start(out=out[r * P : (r + 1) * P, :], in_=result[:])
 
-        for g in range(F_PASSES):
-            regroup_h(0, g)
-        for g in range(F_PASSES):
-            quantise_h(0, g)
-        for s in range(PIECE_LAG + EARLY_TILES * (CHUNKS - 1)):
-            band, place = divmod(s, TILES_PER_BAND)
-            closes_band = band < BANDS and place == TILES_PER_BAND - 1
-            if band < BANDS:
-                sum_rows(s)
-            if closes_band:
-                take_roots(band)
-            c, r = divmod(s - PIECE_LAG, EARLY_TILES)
-            if c >= 0:
-                normalise_piece(r, c)
-            if closes_band:
-                invert_and_spread(band)
-            if 0 < band < BANDS and place == TILES_PER_BAND - 2:
-                keep_row(band - 1)
-
-        def staged(stage, r):
-            if 0 <= r < ROW_TILES:
-                stage(r)
-
-        regroup_h(1, 0)
-        regroup_h(1, 1)
+        vcopy, scopy = nc.vector.tensor_copy, nc.scalar.copy
+        early = {5: (0, 0), 6: (1, 0), 9: (0, 1), 10: (1, 1), 11: (2, 0), 12: (2, 1), 13: (0, 2), 14: (1, 2), 15: (2, 2)}
+        direct = {0: False, 1: True, 3: False, 4: True}
+        regroup_h(0, 0, scopy)
+        regroup_h(1, 0, vcopy)
+        regroup_h(2, 0, gcopy)
+        quantise_h(0, 0)
         quantise_h(1, 0)
-        keep_row(BANDS - 1)
-        regroup_h(2, 1)
-        normalise_rest(0)
-        for k in range(-2, ROW_TILES + 2):
-            staged(finish, k - 2)
-            staged(quantise_agg, k - 1)
-            staged(quantise_rows, k + 1)
-            if k == -1:
-                for c in range(1, CHUNKS):
-                    quantise_h(c, 1)
-            staged(normalise_rest, k + 3)
-            staged(aggregate, k)
-            staged(project, k - 1)
-            staged(turn, k + 2)
-            if k == -2:
-                regroup_h(2, 0)
-                regroup_h(3, 0)
-                regroup_h(3, 1)
+        for s in range(ROW_TILES):
+            if s in direct:
+                sum_direct(s, direct[s])
+            else:
+                sum_folded(s)
+            if s == 0:
+                regroup_h(3, 0, vcopy)
+            if s == 1:
                 quantise_h(2, 0)
                 quantise_h(3, 0)
-            if k == -1:
-                turn_w2()
-            if k == 0:
+            if s % 4 == 3 and s < 15:
+                invert(s - 3, 4)
+            if s % 4 == 0 and s > 0:
+                spread(s - 4, 4)
+                keep_row(s - 4, 4)
+            if s == 14:
+                invert(12, 3)
+            if s == 15:
+                spread(12, 3)
+                invert(15, 1)
+                keep_row(12, 3)
+                spread(15, 1)
+                keep_row(15, 1)
+            if s in early:
+                normalise(*early[s])
+            if s - 1 in early:
+                turn(*early[s - 1])
+            if s - 2 in early:
+                quantise_unit(*early[s - 2])
+        late = [(0, 3), (1, 3), (2, 3)] + [(m, c) for m in range(3, 8) for c in range(CHUNKS)]
+        normalise(*late[0])
+        turn(*early[15])
+        turn(*late[0])
+        quantise_unit(*early[14])
+        quantise_unit(*early[15])
+        normalise(*late[1])
+        regroup_h(0, 1, scopy)
+        quantise_unit(*late[0])
+        turn(*late[1])
+        regroup_h(2, 1, vcopy)
+        regroup_h(1, 1, scopy)
+        quantise_unit(*late[1])
+        quantise_h(0, 1)
+        regroup_h(3, 1, vcopy)
+        quantise_h(2, 1)
+        quantise_h(1, 1)
+        quantise_h(3, 1)
+        slots = [(0, 0), (1, 0), (0, 1), (1, 1)] + [(m, g) for m in range(2, 8) for g in range(2)]
+        done_after = {slots.index((m, 1)): m for m in range(8)}
+        norm_at = {0: [2], 1: [3, 4], 2: [5], 3: [6]}
+        for k in range(4, 12):
+            norm_at[k] = [2 * k - 1, 2 * k]
+        for k in range(len(slots) + 4):
+            if k < len(slots):
+                aggregate(*slots[k])
+            if k - 2 in done_after:
+                project(done_after[k - 2])
+            for i in norm_at.get(k - 1, []):
+                turn(*late[i])
+            if k == 2:
+                turn_w2(0)
+                turn_w2(1)
+            if k == 2 + 1:
                 quantise_w2()
+
+            if k - 1 in done_after:
+                quantise_agg(done_after[k - 1])
+            for i in norm_at.get(k, []):
+                if k >= 0:
+                    normalise(*late[i])
+            for i in norm_at.get(k - 1, []):
+                quantise_unit(*late[i])
+            if k - 3 in done_after:
+                finish(done_after[k - 3])

@@ -36,8 +36,8 @@ def tile_simplegcn_pb_kernel(tc, h, adj, W2, b2, out):
         small = stack.enter_context(tc.tile_pool(name="small", bufs=2))
         h_stage = stack.enter_context(tc.tile_pool(name="h_stage", bufs=5))
         u_stage = stack.enter_context(tc.tile_pool(name="u_stage", bufs=4))
-        a_stage = stack.enter_context(tc.tile_pool(name="a_stage", bufs=4))
-        g_stage = stack.enter_context(tc.tile_pool(name="g_stage", bufs=3))
+        a_stage = stack.enter_context(tc.tile_pool(name="a_stage", bufs=5))
+        g_stage = stack.enter_context(tc.tile_pool(name="g_stage", bufs=8))
         o_stage = stack.enter_context(tc.tile_pool(name="o_stage", bufs=4))
         turn_psum = stack.enter_context(tc.psum_pool(name="turn_psum", bufs=2))
         agg_psum = stack.enter_context(tc.psum_pool(name="agg_psum", bufs=4))
@@ -63,6 +63,8 @@ def tile_simplegcn_pb_kernel(tc, h, adj, W2, b2, out):
         w2_scales = keep.tile([P, F_PASSES, OUT], U8, align_bytes=64)
 
         nc.gpsimd.memset(eps_col[:], EPS)
+        first_root = keep.tile([P, 1], F32)
+        nc.scalar.activation(out=first_root[:], in_=eps_col[:], func=ACT.Abs_reciprocal_sqrt)
         make_identity(nc, ident_bf16[:])
         make_identity(nc, ident_f32[:])
 
@@ -75,12 +77,14 @@ def tile_simplegcn_pb_kernel(tc, h, adj, W2, b2, out):
                     in_=h[j0 : j0 + K_PASS // 2, cols].rearrange("(p e) f -> p e f", e=2),
                 )
 
-        load_h(0, 0)
-        load_h(1, 0)
-        load_h(2, 0)
-        load_h(3, 0)
+        h_after = {3: 2, 7: 3}
+        for c in range(CHUNKS):
+            if c not in h_after.values():
+                load_h(c, 0)
         for r in range(ROW_TILES - 1):
             nc.sync.dma_start(out=adj_rows[:, r, :], in_=adj[r * P : (r + 1) * P, :])
+            if r in h_after:
+                load_h(h_after[r], 0)
         for half in range(2):
             cols = slice(half * NODES // 2, (half + 1) * NODES // 2)
             nc.sync.dma_start(out=adj_rows[:, ROW_TILES - 1, cols], in_=adj[NODES - P :, cols])
@@ -89,15 +93,20 @@ def tile_simplegcn_pb_kernel(tc, h, adj, W2, b2, out):
         nc.sync.dma_start(out=w2_rows[:], in_=W2.rearrange("(b p) f -> p b f", p=P))
         nc.sync.dma_start(out=bias_rows[:], in_=b2.partition_broadcast(P))
 
+        w2_banks = {}
+
         def turn_w2(g):
             w2_turned = out_psum.tile([P, O_TILES, PACK, P], BF16, tag="out")
             for b in range(O_TILES):
                 for t in range(PACK):
                     f0 = g * K_PASS + t * P
                     nc.tensor.transpose(w2_turned[:, b, t, :], w2_rows[:, b, f0 : f0 + P], ident_bf16[:])
+            w2_banks[g] = w2_turned
+
+        def group_w2(g):
             nc.scalar.copy(
                 out=w2_grouped[:, g, :, :].rearrange("p (b o) t -> p b o t", b=O_TILES),
-                in_=w2_turned[:].rearrange("p b t o -> p b o t"),
+                in_=w2_banks[g][:].rearrange("p b t o -> p b o t"),
             )
 
         def quantise_w2():
@@ -146,7 +155,9 @@ def tile_simplegcn_pb_kernel(tc, h, adj, W2, b2, out):
                     out=unused_scalar[:], in_=adj_rows[:, r, :], func=ACT.Copy, accum_out=deg[:, r, 0:1]
                 )
 
-        def sum_folded(r):
+        folded_banks = {}
+
+        def fold(r):
             folded = agg_psum.tile([P, SUM_WIDTH], F32, tag="agg")
             for n in range(NODES // SUM_WIDTH):
                 nc.tensor.matmul(
@@ -156,8 +167,13 @@ def tile_simplegcn_pb_kernel(tc, h, adj, W2, b2, out):
                     start=(n == 0),
                     stop=(n == NODES // SUM_WIDTH - 1),
                 )
+            folded_banks[r] = folded
+
+        def reduce(r):
             unused_folded = small.tile([P, SUM_WIDTH], BF16)
-            nc.scalar.activation(out=unused_folded[:], in_=folded[:], func=ACT.Copy, accum_out=deg[:, r, 0:1])
+            nc.scalar.activation(
+                out=unused_folded[:], in_=folded_banks[r][:], func=ACT.Copy, accum_out=deg[:, r, 0:1]
+            )
 
         def invert(r0, n):
             nc.scalar.activation(
@@ -181,6 +197,7 @@ def tile_simplegcn_pb_kernel(tc, h, adj, W2, b2, out):
 
         row_operands = {}
         unit_values = {}
+        turned_banks = {}
 
         def normalise(m, c):
             cols = slice(c * K_PASS, (c + 1) * K_PASS)
@@ -203,9 +220,12 @@ def tile_simplegcn_pb_kernel(tc, h, adj, W2, b2, out):
                 for u in range(2):
                     w0 = c * (K_PASS // 2) + u * P
                     nc.tensor.transpose(turned[:, place, u, :], words[:, w0 : w0 + P], ident_f32[:])
+            turned_banks[(m, c)] = turned
+
+        def group_unit(m, c):
             nc.scalar.copy(
-                out=grouped[:].bitcast(F32).rearrange("p (l i u) -> p l i u", l=2, u=2),
-                in_=turned[:].rearrange("p l u i -> p l i u"),
+                out=unit_values[(m, c)][:].bitcast(F32).rearrange("p (l i u) -> p l i u", l=2, u=2),
+                in_=turned_banks[(m, c)][:].rearrange("p l u i -> p l i u"),
             )
 
         def quantise_unit(m, c):
@@ -218,88 +238,97 @@ def tile_simplegcn_pb_kernel(tc, h, adj, W2, b2, out):
                 out=a_codes[:, c, :].bitcast(FP8X4), scales=a_scales[:, c, :], in_=unit_values[(m, c)][:]
             )
 
+        agg_banks = {}
         g_values = {}
         g_operands = {}
         out_banks = {}
 
-        def aggregate(m, g):
-            if m not in g_values:
-                agg_grouped = g_stage.tile([P, F_PASSES, 2 * P, PACK], BF16, align_bytes=64)
-                g_values[m] = agg_grouped
-            a_codes, a_scales = row_operands[m]
-            for q in range(2):
-                agg_t = agg_psum.tile([P, 2, 2 * P], F32, tag="agg")
-                for s in range(2):
-                    f0 = g * K_PASS + (2 * q + s) * P
-                    for c in range(CHUNKS):
-                        nc.tensor.matmul_mx(
-                            out=agg_t[:, s, :],
-                            lhsT=h_codes[:, c, f0 : f0 + P].bitcast(FP8X4),
-                            lhsT_scale=h_scales[:, c, f0 : f0 + P],
-                            rhs=a_codes[:, c, :].bitcast(FP8X4),
-                            rhs_scale=a_scales[:, c, :],
-                            start=(c == 0),
-                            stop=(c == CHUNKS - 1),
-                        )
-                nc.scalar.copy(out=g_values[m][:, g, :, 2 * q : 2 * q + 2], in_=agg_t[:].rearrange("p s i -> p i s"))
+        def aggregate(r, g):
+            if r not in g_values:
+                agg_grouped = g_stage.tile([P, F_PASSES, P, PACK], BF16, align_bytes=64)
+                g_values[r] = agg_grouped
+            a_codes, a_scales = row_operands[r // 2]
+            cols = slice((r % 2) * P, (r % 2 + 1) * P)
+            agg_t = agg_psum.tile([P, PACK, P], F32, tag="agg")
+            agg_banks[(r, g)] = agg_t
+            for t in range(PACK):
+                f0 = g * K_PASS + t * P
+                for c in range(CHUNKS):
+                    nc.tensor.matmul_mx(
+                        out=agg_t[:, t, :],
+                        lhsT=h_codes[:, c, f0 : f0 + P].bitcast(FP8X4),
+                        lhsT_scale=h_scales[:, c, f0 : f0 + P],
+                        rhs=a_codes[:, c, cols].bitcast(FP8X4),
+                        rhs_scale=a_scales[:, c, cols],
+                        start=(c == 0),
+                        stop=(c == CHUNKS - 1),
+                    )
 
-        def quantise_agg(m):
-            agg_codes = g_stage.tile([P, F_PASSES, 2 * P], U32, align_bytes=64)
-            agg_scales = g_stage.tile([P, F_PASSES, 2 * P], U8, align_bytes=64)
-            g_operands[m] = (agg_codes, agg_scales)
+        def group_agg(r, g):
+            nc.scalar.copy(out=g_values[r][:, g, :, :], in_=agg_banks[(r, g)][:].rearrange("p t i -> p i t"))
+
+        def quantise_agg(r):
+            agg_codes = g_stage.tile([P, F_PASSES, P], U32, align_bytes=64)
+            agg_scales = g_stage.tile([P, F_PASSES, P], U8, align_bytes=64)
+            g_operands[r] = (agg_codes, agg_scales)
             nc.vector.quantize_mx(
                 out=agg_codes[:].rearrange("p g i -> p (g i)").bitcast(FP8X4),
                 scales=agg_scales[:].rearrange("p g i -> p (g i)"),
-                in_=g_values[m][:].rearrange("p g i t -> p (g i t)"),
+                in_=g_values[r][:].rearrange("p g i t -> p (g i t)"),
             )
 
-        def project(m):
-            agg_codes, agg_scales = g_operands[m]
-            out_rows = out_psum.tile([P, 2, OUT], F32, tag="out")
-            out_banks[m] = out_rows
-            for place in range(2):
-                cols = slice(place * P, (place + 1) * P)
-                for g in range(F_PASSES):
-                    nc.tensor.matmul_mx(
-                        out=out_rows[:, place, :],
-                        lhsT=agg_codes[:, g, cols].bitcast(FP8X4),
-                        lhsT_scale=agg_scales[:, g, cols],
-                        rhs=w2_codes[:, g, :].bitcast(FP8X4),
-                        rhs_scale=w2_scales[:, g, :],
-                        start=(g == 0),
-                        stop=(g == F_PASSES - 1),
-                    )
+        def project(r):
+            agg_codes, agg_scales = g_operands[r]
+            out_rows = out_psum.tile([P, OUT], F32, tag="out")
+            out_banks[r] = out_rows
+            for g in range(F_PASSES):
+                nc.tensor.matmul_mx(
+                    out=out_rows[:],
+                    lhsT=agg_codes[:, g, :].bitcast(FP8X4),
+                    lhsT_scale=agg_scales[:, g, :],
+                    rhs=w2_codes[:, g, :].bitcast(FP8X4),
+                    rhs_scale=w2_scales[:, g, :],
+                    start=(g == 0),
+                    stop=(g == F_PASSES - 1),
+                )
 
-        def finish(m):
-            for place in range(2):
-                r = 2 * m + place
-                result = o_stage.tile([P, OUT], F32)
-                nc.vector.tensor_tensor(out=result[:], in0=out_banks[m][:, place, :], in1=bias_rows[:], op=ALU.add)
-                nc.sync.dma_start(out=out[r * P : (r + 1) * P, :], in_=result[:])
+        def finish(r):
+            result = o_stage.tile([P, OUT], F32)
+            nc.vector.tensor_tensor(out=result[:], in0=out_banks[r][:], in1=bias_rows[:], op=ALU.add)
+            nc.sync.dma_start(out=out[r * P : (r + 1) * P, :], in_=result[:])
 
         vcopy, scopy = nc.vector.tensor_copy, nc.scalar.copy
-        early = {5: (0, 0), 6: (1, 0), 9: (0, 1), 10: (1, 1), 11: (2, 0), 12: (2, 1), 13: (0, 2), 14: (1, 2), 15: (2, 2)}
-        direct = {0: False, 1: True, 3: False, 4: True}
-        regroup_h(0, 0, scopy)
-        regroup_h(1, 0, vcopy)
-        regroup_h(2, 0, gcopy)
+        early = {5: ((0, 0),), 6: ((1, 0),), 9: ((0, 1),), 10: ((1, 1),), 11: ((2, 0),), 12: ((2, 1),), 13: ((0, 2),), 14: ((1, 2),), 15: ((2, 2),)}
+        on_vector = (1, 2)
+        on_scalar = (0,)
+        last_of_band = (3, 7, 11)
+        regroup_h(0, 0, vcopy)
+        regroup_h(1, 0, scopy)
         quantise_h(0, 0)
-        quantise_h(1, 0)
         for s in range(ROW_TILES):
-            if s in direct:
-                sum_direct(s, direct[s])
+            if s in on_vector:
+                sum_direct(s, True)
+            elif s in on_scalar:
+                sum_direct(s, False)
             else:
-                sum_folded(s)
-            if s == 0:
-                regroup_h(3, 0, vcopy)
-            if s == 1:
-                quantise_h(2, 0)
-                quantise_h(3, 0)
-            if s % 4 == 3 and s < 15:
-                invert(s - 3, 4)
-            if s % 4 == 0 and s > 0:
+                fold(s)
+            if s - 1 in last_of_band:
                 spread(s - 4, 4)
                 keep_row(s - 4, 4)
+            if s not in on_vector and s not in on_scalar:
+                reduce(s)
+            if s in last_of_band:
+                invert(s - 3, 4)
+            if s == 2:
+                quantise_h(1, 0)
+            if s == 3:
+                regroup_h(2, 0, vcopy)
+            if s == 4:
+                quantise_h(2, 0)
+            if s == 7:
+                regroup_h(3, 0, vcopy)
+            if s == 8:
+                quantise_h(3, 0)
             if s == 14:
                 invert(12, 3)
             if s == 15:
@@ -308,54 +337,65 @@ def tile_simplegcn_pb_kernel(tc, h, adj, W2, b2, out):
                 keep_row(12, 3)
                 spread(15, 1)
                 keep_row(15, 1)
-            if s in early:
-                normalise(*early[s])
-            if s - 1 in early:
-                turn(*early[s - 1])
-            if s - 2 in early:
-                quantise_unit(*early[s - 2])
+            for u in early.get(s, ()):
+                normalise(*u)
+            for u in early.get(s - 1, ()):
+                turn(*u)
+                group_unit(*u)
+            for u in early.get(s - 2, ()):
+                quantise_unit(*u)
         late = [(0, 3), (1, 3), (2, 3)] + [(m, c) for m in range(3, 8) for c in range(CHUNKS)]
+        turn(*early[15][0])
+        group_unit(*early[15][0])
         normalise(*late[0])
-        turn(*early[15])
+        quantise_unit(*early[14][0])
         turn(*late[0])
-        quantise_unit(*early[14])
-        quantise_unit(*early[15])
+        group_unit(*late[0])
+        quantise_unit(*early[15][0])
         normalise(*late[1])
         regroup_h(0, 1, scopy)
         quantise_unit(*late[0])
         turn(*late[1])
-        regroup_h(2, 1, vcopy)
-        regroup_h(1, 1, scopy)
+        group_unit(*late[1])
+        normalise(*late[2])
         quantise_unit(*late[1])
+        turn(*late[2])
+        regroup_h(2, 1, vcopy)
+        group_unit(*late[2])
+        regroup_h(1, 1, scopy)
         quantise_h(0, 1)
+        quantise_unit(*late[2])
         regroup_h(3, 1, vcopy)
         quantise_h(2, 1)
         quantise_h(1, 1)
         quantise_h(3, 1)
-        slots = [(0, 0), (1, 0), (0, 1), (1, 1)] + [(m, g) for m in range(2, 8) for g in range(2)]
-        done_after = {slots.index((m, 1)): m for m in range(8)}
-        norm_at = {0: [2], 1: [3, 4], 2: [5], 3: [6]}
-        for k in range(4, 12):
-            norm_at[k] = [2 * k - 1, 2 * k]
-        for k in range(len(slots) + 4):
+        slots = [(r, g) for g in range(2) for r in range(6)] + [(r, g) for r in range(6, 16) for g in range(2)]
+        done_after = {slots.index((r, 1)): r for r in range(16)}
+        norm_at = {}
+        for i in range(3, len(late)):
+            norm_at[6 + 2 * ((i - 3) // 2)] = [j for j in (i - (i - 3) % 2, i - (i - 3) % 2 + 1) if j < len(late)]
+        for k in range(len(slots) + 5):
             if k < len(slots):
                 aggregate(*slots[k])
+                group_agg(*slots[k])
             if k - 2 in done_after:
                 project(done_after[k - 2])
             for i in norm_at.get(k - 1, []):
                 turn(*late[i])
-            if k == 2:
+                group_unit(*late[i])
+            if k == 5:
                 turn_w2(0)
                 turn_w2(1)
-            if k == 2 + 1:
+                group_w2(0)
+                group_w2(1)
+            if k == 5 + 2:
                 quantise_w2()
 
             if k - 1 in done_after:
                 quantise_agg(done_after[k - 1])
             for i in norm_at.get(k, []):
-                if k >= 0:
-                    normalise(*late[i])
-            for i in norm_at.get(k - 1, []):
+                normalise(*late[i])
+            for i in norm_at.get(k - 2, []):
                 quantise_unit(*late[i])
             if k - 3 in done_after:
                 finish(done_after[k - 3])

@@ -24,7 +24,7 @@ ROW_TILES = NODES // P
 CHUNKS = NODES // K_PASS
 F_PASSES = HID // K_PASS
 O_TILES = OUT // P
-SUM_WIDTH = 256
+SUM_WIDTH = 512
 
 FLOPS = 2 * NODES * NODES * HID + 2 * NODES * HID * OUT
 

@@ -37,11 +37,11 @@ def tile_simplegcn_pb_kernel(tc, h, adj, W2, b2, out):
         h_stage = stack.enter_context(tc.tile_pool(name="h_stage", bufs=5))
         u_stage = stack.enter_context(tc.tile_pool(name="u_stage", bufs=4))
         a_stage = stack.enter_context(tc.tile_pool(name="a_stage", bufs=5))
-        g_stage = stack.enter_context(tc.tile_pool(name="g_stage", bufs=8))
-        o_stage = stack.enter_context(tc.tile_pool(name="o_stage", bufs=4))
-        turn_psum = stack.enter_context(tc.psum_pool(name="turn_psum", bufs=2))
-        agg_psum = stack.enter_context(tc.psum_pool(name="agg_psum", bufs=4))
-        out_psum = stack.enter_context(tc.psum_pool(name="out_psum", bufs=2))
+        g_stage = stack.enter_context(tc.tile_pool(name="g_stage", bufs=4))
+        o_stage = stack.enter_context(tc.tile_pool(name="o_stage", bufs=2))
+        turn_psum = stack.enter_context(tc.psum_pool(name="turn_psum", bufs=4))
+        agg_psum = stack.enter_context(tc.psum_pool(name="agg_psum", bufs=3))
+        out_psum = stack.enter_context(tc.psum_pool(name="out_psum", bufs=1))
         stack.enter_context(tc.manual_schedule())
 
         ident_f32 = keep.tile([P, P], F32)
@@ -51,7 +51,7 @@ def tile_simplegcn_pb_kernel(tc, h, adj, W2, b2, out):
         h_rows_1 = keep.tile([P, CHUNKS, PACK, K_PASS], BF16)
         h_rows = (h_rows_0, h_rows_1)
         adj_rows = keep.tile([P, ROW_TILES, NODES], BF16)
-        bias_rows = keep.tile([P, OUT], BF16)
+        bias_rows = keep.tile([P, 2, OUT], BF16)
         deg = keep.tile([P, ROW_TILES, 8], F32)
         eps_col = keep.tile([P, 1], F32)
         d_col = keep.tile([P, ROW_TILES], F32)
@@ -79,7 +79,7 @@ def tile_simplegcn_pb_kernel(tc, h, adj, W2, b2, out):
 
         h_after = {3: 2, 7: 3}
         for c in range(CHUNKS):
-            if c not in h_after.values():
+            if c not in h_after.values() and c < 2:
                 load_h(c, 0)
         for r in range(ROW_TILES - 1):
             nc.sync.dma_start(out=adj_rows[:, r, :], in_=adj[r * P : (r + 1) * P, :])
@@ -88,15 +88,19 @@ def tile_simplegcn_pb_kernel(tc, h, adj, W2, b2, out):
         for half in range(2):
             cols = slice(half * NODES // 2, (half + 1) * NODES // 2)
             nc.sync.dma_start(out=adj_rows[:, ROW_TILES - 1, cols], in_=adj[NODES - P :, cols])
+        for c in range(2, CHUNKS):
+            if c not in h_after.values():
+                load_h(c, 0)
         for c in range(CHUNKS):
             load_h(c, 1)
         nc.sync.dma_start(out=w2_rows[:], in_=W2.rearrange("(b p) f -> p b f", p=P))
-        nc.sync.dma_start(out=bias_rows[:], in_=b2.partition_broadcast(P))
+        nc.sync.dma_start(out=bias_rows[:, 0, :], in_=b2.partition_broadcast(P))
+        nc.gpsimd.tensor_copy(out=bias_rows[:, 1, :], in_=bias_rows[:, 0, :])
 
         w2_banks = {}
 
         def turn_w2(g):
-            w2_turned = out_psum.tile([P, O_TILES, PACK, P], BF16, tag="out")
+            w2_turned = turn_psum.tile([P, O_TILES, PACK, P], BF16, tag="turn")
             for b in range(O_TILES):
                 for t in range(PACK):
                     f0 = g * K_PASS + t * P
@@ -121,13 +125,19 @@ def tile_simplegcn_pb_kernel(tc, h, adj, W2, b2, out):
         def gcopy(out, in_):
             nc.gpsimd.tensor_scalar(out=out, in0=in_, scalar1=1.0, scalar2=0.0, op0=ALU.mult, op1=ALU.add)
 
-        def regroup_h(c, g, copy):
-            h_grouped = h_stage.tile([P, K_PASS, PACK], BF16, align_bytes=64)
-            h_values[(c, g)] = h_grouped
-            copy(
-                out=h_grouped[:].rearrange("p (a i) t -> p a t i", i=4),
-                in_=h_rows[g][:, c, :, :].rearrange("p t (a i) -> p a t i", i=4),
-            )
+        def regroup_h(c, g, copy, pieces=(0, 1, 2, 3)):
+            if (c, g) not in h_values:
+                h_grouped = h_stage.tile([P, K_PASS, PACK], BF16, align_bytes=64)
+                h_values[(c, g)] = h_grouped
+            if len(pieces) == 4:
+                spans = [(0, K_PASS)]
+            else:
+                spans = [(q * P, (q + 1) * P) for q in pieces]
+            for f0, f1 in spans:
+                copy(
+                    out=h_values[(c, g)][:, f0:f1, :].rearrange("p (a i) t -> p a t i", i=4),
+                    in_=h_rows[g][:, c, :, f0:f1].rearrange("p t (a i) -> p a t i", i=4),
+                )
 
         def quantise_h(c, g):
             cols = slice(g * K_PASS, (g + 1) * K_PASS)
@@ -183,7 +193,7 @@ def tile_simplegcn_pb_kernel(tc, h, adj, W2, b2, out):
         spread_banks = {}
 
         def spread(r0, n):
-            bank = out_psum.tile([P, PACK, P], F32, tag="out")
+            bank = agg_psum.tile([P, PACK, P], F32, tag="agg")
             for place in range(n):
                 r = r0 + place
                 nc.tensor.transpose(bank[:, place, :], d_col[:, r : r + 1].to_broadcast([P, P]), ident_f32[:])
@@ -199,43 +209,56 @@ def tile_simplegcn_pb_kernel(tc, h, adj, W2, b2, out):
         unit_values = {}
         turned_banks = {}
 
-        def normalise(m, c):
-            cols = slice(c * K_PASS, (c + 1) * K_PASS)
-            for r in (2 * m, 2 * m + 1):
-                nc.vector.scalar_tensor_tensor(
-                    out=adj_rows[:, r, cols],
-                    in0=adj_rows[:, r, cols],
-                    scalar=d_col[:, r : r + 1],
-                    in1=d_row[:, cols],
-                    op0=ALU.mult,
-                    op1=ALU.mult,
-                )
+        def normalise(r, c, width):
+            cols = slice(c * K_PASS, (c + width) * K_PASS)
+            nc.vector.scalar_tensor_tensor(
+                out=adj_rows[:, r, cols],
+                in0=adj_rows[:, r, cols],
+                scalar=d_col[:, r : r + 1],
+                in1=d_row[:, cols],
+                op0=ALU.mult,
+                op1=ALU.mult,
+            )
+
+        def norm_unit(m, c):
+            normalise(2 * m, c, 1)
+            normalise(2 * m + 1, c, 1)
 
         def turn(m, c):
             turned = turn_psum.tile([P, 2, 2, P], F32, tag="turn")
-            grouped = u_stage.tile([P, 2 * K_PASS], BF16, align_bytes=64)
-            unit_values[(m, c)] = grouped
+            turned_banks[(m, c)] = turned
             for place in range(2):
                 words = adj_rows[:, 2 * m + place, :].bitcast(F32)
                 for u in range(2):
                     w0 = c * (K_PASS // 2) + u * P
                     nc.tensor.transpose(turned[:, place, u, :], words[:, w0 : w0 + P], ident_f32[:])
-            turned_banks[(m, c)] = turned
+
+        def new_values(m, c, width):
+            grouped = u_stage.tile([P, width * 2 * K_PASS], BF16, align_bytes=64, tag="grouped_%d" % width, bufs=width == 1 and 4 or 3)
+            for n in range(width):
+                unit_values[(m, c + n)] = (grouped, n)
 
         def group_unit(m, c):
+            if (m, c) not in unit_values:
+                new_values(m, c, 1)
+            grouped, n = unit_values[(m, c)]
             nc.scalar.copy(
-                out=unit_values[(m, c)][:].bitcast(F32).rearrange("p (l i u) -> p l i u", l=2, u=2),
+                out=grouped[:, n * 2 * K_PASS : (n + 1) * 2 * K_PASS]
+                .bitcast(F32)
+                .rearrange("p (l i u) -> p l i u", l=2, u=2),
                 in_=turned_banks[(m, c)][:].rearrange("p l u i -> p l i u"),
             )
 
-        def quantise_unit(m, c):
+        def quantise(m, c, width):
             if m not in row_operands:
                 a_codes = a_stage.tile([P, CHUNKS, 2 * P], U32, align_bytes=64)
                 a_scales = a_stage.tile([P, CHUNKS, 2 * P], U8, align_bytes=64)
                 row_operands[m] = (a_codes, a_scales)
             a_codes, a_scales = row_operands[m]
             nc.vector.quantize_mx(
-                out=a_codes[:, c, :].bitcast(FP8X4), scales=a_scales[:, c, :], in_=unit_values[(m, c)][:]
+                out=a_codes[:, c : c + width, :].rearrange("p c i -> p (c i)").bitcast(FP8X4),
+                scales=a_scales[:, c : c + width, :].rearrange("p c i -> p (c i)"),
+                in_=unit_values[(m, c)][0][:],
             )
 
         agg_banks = {}
@@ -243,66 +266,77 @@ def tile_simplegcn_pb_kernel(tc, h, adj, W2, b2, out):
         g_operands = {}
         out_banks = {}
 
-        def aggregate(r, g):
-            if r not in g_values:
-                agg_grouped = g_stage.tile([P, F_PASSES, P, PACK], BF16, align_bytes=64)
-                g_values[r] = agg_grouped
-            a_codes, a_scales = row_operands[r // 2]
-            cols = slice((r % 2) * P, (r % 2 + 1) * P)
-            agg_t = agg_psum.tile([P, PACK, P], F32, tag="agg")
-            agg_banks[(r, g)] = agg_t
-            for t in range(PACK):
-                f0 = g * K_PASS + t * P
-                for c in range(CHUNKS):
-                    nc.tensor.matmul_mx(
-                        out=agg_t[:, t, :],
-                        lhsT=h_codes[:, c, f0 : f0 + P].bitcast(FP8X4),
-                        lhsT_scale=h_scales[:, c, f0 : f0 + P],
-                        rhs=a_codes[:, c, cols].bitcast(FP8X4),
-                        rhs_scale=a_scales[:, c, cols],
-                        start=(c == 0),
-                        stop=(c == CHUNKS - 1),
-                    )
+        def aggregate(m, g):
+            if m not in g_values:
+                agg_grouped = g_stage.tile([P, F_PASSES, 2 * P, PACK], BF16, align_bytes=64)
+                g_values[m] = agg_grouped
+            a_codes, a_scales = row_operands[m]
+            for q in range(2):
+                agg_t = agg_psum.tile([P, 2, 2 * P], F32, tag="agg")
+                for s in range(2):
+                    f0 = g * K_PASS + (2 * q + s) * P
+                    for c in range(CHUNKS):
+                        nc.tensor.matmul_mx(
+                            out=agg_t[:, s, :],
+                            lhsT=h_codes[:, c, f0 : f0 + P].bitcast(FP8X4),
+                            lhsT_scale=h_scales[:, c, f0 : f0 + P],
+                            rhs=a_codes[:, c, :].bitcast(FP8X4),
+                            rhs_scale=a_scales[:, c, :],
+                            start=(c == 0),
+                            stop=(c == CHUNKS - 1),
+                        )
+                agg_banks[(m, g, q)] = agg_t
 
-        def group_agg(r, g):
-            nc.scalar.copy(out=g_values[r][:, g, :, :], in_=agg_banks[(r, g)][:].rearrange("p t i -> p i t"))
+        def group_agg(m, g):
+            for q in range(2):
+                nc.scalar.copy(
+                    out=g_values[m][:, g, :, 2 * q : 2 * q + 2],
+                    in_=agg_banks[(m, g, q)][:].rearrange("p s i -> p i s"),
+                )
 
-        def quantise_agg(r):
-            agg_codes = g_stage.tile([P, F_PASSES, P], U32, align_bytes=64)
-            agg_scales = g_stage.tile([P, F_PASSES, P], U8, align_bytes=64)
-            g_operands[r] = (agg_codes, agg_scales)
+        def quantise_agg(m):
+            agg_codes = g_stage.tile([P, F_PASSES, 2 * P], U32, align_bytes=64, bufs=2)
+            agg_scales = g_stage.tile([P, F_PASSES, 2 * P], U8, align_bytes=64, bufs=2)
+            g_operands[m] = (agg_codes, agg_scales)
             nc.vector.quantize_mx(
                 out=agg_codes[:].rearrange("p g i -> p (g i)").bitcast(FP8X4),
                 scales=agg_scales[:].rearrange("p g i -> p (g i)"),
-                in_=g_values[r][:].rearrange("p g i t -> p (g i t)"),
+                in_=g_values[m][:].rearrange("p g i t -> p (g i t)"),
             )
 
-        def project(r):
-            agg_codes, agg_scales = g_operands[r]
-            out_rows = out_psum.tile([P, OUT], F32, tag="out")
-            out_banks[r] = out_rows
-            for g in range(F_PASSES):
-                nc.tensor.matmul_mx(
-                    out=out_rows[:],
-                    lhsT=agg_codes[:, g, :].bitcast(FP8X4),
-                    lhsT_scale=agg_scales[:, g, :],
-                    rhs=w2_codes[:, g, :].bitcast(FP8X4),
-                    rhs_scale=w2_scales[:, g, :],
-                    start=(g == 0),
-                    stop=(g == F_PASSES - 1),
-                )
+        def project(m):
+            agg_codes, agg_scales = g_operands[m]
+            out_rows = out_psum.tile([P, 2, OUT], F32, tag="out")
+            out_banks[m] = out_rows
+            for place in range(2):
+                cols = slice(place * P, (place + 1) * P)
+                for g in range(F_PASSES):
+                    nc.tensor.matmul_mx(
+                        out=out_rows[:, place, :],
+                        lhsT=agg_codes[:, g, cols].bitcast(FP8X4),
+                        lhsT_scale=agg_scales[:, g, cols],
+                        rhs=w2_codes[:, g, :].bitcast(FP8X4),
+                        rhs_scale=w2_scales[:, g, :],
+                        start=(g == 0),
+                        stop=(g == F_PASSES - 1),
+                    )
 
-        def finish(r):
-            result = o_stage.tile([P, OUT], F32)
-            nc.vector.tensor_tensor(out=result[:], in0=out_banks[r][:], in1=bias_rows[:], op=ALU.add)
-            nc.sync.dma_start(out=out[r * P : (r + 1) * P, :], in_=result[:])
+        def finish(m):
+            result = o_stage.tile([P, 2, OUT], F32)
+            nc.vector.tensor_tensor(out=result[:], in0=out_banks[m][:], in1=bias_rows[:], op=ALU.add)
+            nc.sync.dma_start(
+                out=out[2 * m * P : 2 * (m + 1) * P, :].rearrange("(l p) o -> p l o", l=2), in_=result[:]
+            )
 
         vcopy, scopy = nc.vector.tensor_copy, nc.scalar.copy
-        early = {5: ((0, 0),), 6: ((1, 0),), 9: ((0, 1),), 10: ((1, 1),), 11: ((2, 0),), 12: ((2, 1),), 13: ((0, 2),), 14: ((1, 2),), 15: ((2, 2),)}
-        on_vector = (1, 2)
-        on_scalar = (0,)
-        last_of_band = (3, 7, 11)
-        regroup_h(0, 0, vcopy)
+        on_vector = (0, 1)
+        on_scalar = ()
+        norm_at = {5: (0, 0), 6: (1, 0), 9: (0, 1), 10: (1, 1), 11: (2, 0), 12: (2, 1), 13: (0, 2), 14: (1, 2), 15: (2, 2)}
+        turn_at = {7: (0, 0), 8: (1, 0), 11: (0, 1), 12: (1, 1), 14: (2, 0)}
+        quant_at = {8: (0, 0), 9: (1, 0), 12: (0, 1), 13: (1, 1), 15: (2, 0)}
+        piece_at = {}
+        hq_at = {2: 1, 5: 2, 9: 3}
+        regroup_h(0, 0, scopy)
         regroup_h(1, 0, scopy)
         quantise_h(0, 0)
         for s in range(ROW_TILES):
@@ -312,90 +346,113 @@ def tile_simplegcn_pb_kernel(tc, h, adj, W2, b2, out):
                 sum_direct(s, False)
             else:
                 fold(s)
-            if s - 1 in last_of_band:
+            if s in (4, 8, 12):
                 spread(s - 4, 4)
-                keep_row(s - 4, 4)
+            if s == 15:
+                spread(12, 3)
             if s not in on_vector and s not in on_scalar:
                 reduce(s)
-            if s in last_of_band:
+            if s in (4, 8, 12):
+                keep_row(s - 4, 4)
+            if s in (3, 7, 11):
                 invert(s - 3, 4)
-            if s == 2:
-                quantise_h(1, 0)
-            if s == 3:
-                regroup_h(2, 0, vcopy)
-            if s == 4:
-                quantise_h(2, 0)
-            if s == 7:
-                regroup_h(3, 0, vcopy)
-            if s == 8:
-                quantise_h(3, 0)
             if s == 14:
                 invert(12, 3)
             if s == 15:
-                spread(12, 3)
                 invert(15, 1)
                 keep_row(12, 3)
-                spread(15, 1)
-                keep_row(15, 1)
-            for u in early.get(s, ()):
-                normalise(*u)
-            for u in early.get(s - 1, ()):
-                turn(*u)
-                group_unit(*u)
-            for u in early.get(s - 2, ()):
-                quantise_unit(*u)
-        late = [(0, 3), (1, 3), (2, 3)] + [(m, c) for m in range(3, 8) for c in range(CHUNKS)]
-        turn(*early[15][0])
-        group_unit(*early[15][0])
-        normalise(*late[0])
-        quantise_unit(*early[14][0])
-        turn(*late[0])
-        group_unit(*late[0])
-        quantise_unit(*early[15][0])
-        normalise(*late[1])
-        regroup_h(0, 1, scopy)
-        quantise_unit(*late[0])
-        turn(*late[1])
-        group_unit(*late[1])
-        normalise(*late[2])
-        quantise_unit(*late[1])
-        turn(*late[2])
-        regroup_h(2, 1, vcopy)
-        group_unit(*late[2])
-        regroup_h(1, 1, scopy)
-        quantise_h(0, 1)
-        quantise_unit(*late[2])
-        regroup_h(3, 1, vcopy)
-        quantise_h(2, 1)
+            for c, g, pieces in piece_at.get(s, ()):
+                regroup_h(c, g, scopy, pieces)
+            if s == 4:
+                regroup_h(2, 0, vcopy)
+            if s == 8:
+                regroup_h(3, 0, vcopy)
+            if s in norm_at:
+                norm_unit(*norm_at[s])
+            if s in turn_at:
+                turn(*turn_at[s])
+                group_unit(*turn_at[s])
+            if s in quant_at:
+                quantise(*quant_at[s], 1)
+            if s in hq_at:
+                quantise_h(hq_at[s], 0)
+        spread(15, 1)
+        keep_row(15, 1)
+        turn(2, 1)
+        group_unit(2, 1)
+        turn(0, 2)
+        group_unit(0, 2)
+        turn(1, 2)
+        norm_unit(0, 3)
+        turn(0, 3)
+        group_unit(0, 3)
+        group_unit(1, 2)
+        quantise(0, 2, 1)
+        norm_unit(1, 3)
+        quantise(0, 3, 1)
+        turn(2, 2)
+        turn(1, 3)
+        group_unit(1, 3)
+        group_unit(2, 2)
+        quantise(1, 2, 1)
+        quantise(2, 1, 1)
+        norm_unit(2, 3)
+        quantise(1, 3, 1)
+        regroup_h(0, 1, scopy, (0, 1))
+        quantise(2, 2, 1)
+        regroup_h(1, 1, vcopy)
+        regroup_h(0, 1, scopy, (2, 3))
         quantise_h(1, 1)
-        quantise_h(3, 1)
-        slots = [(r, g) for g in range(2) for r in range(6)] + [(r, g) for r in range(6, 16) for g in range(2)]
-        done_after = {slots.index((r, 1)): r for r in range(16)}
-        norm_at = {}
-        for i in range(3, len(late)):
-            norm_at[6 + 2 * ((i - 3) // 2)] = [j for j in (i - (i - 3) % 2, i - (i - 3) % 2 + 1) if j < len(late)]
-        for k in range(len(slots) + 5):
+        regroup_h(2, 1, vcopy)
+        slots = [(m, g) for g in range(2) for m in range(3)] + [(m, g) for m in range(3, 8) for g in range(2)]
+        last_slot = {m: slots.index((m, 1)) for m in range(8)}
+        for k in range(len(slots) + 4):
             if k < len(slots):
                 aggregate(*slots[k])
                 group_agg(*slots[k])
-            if k - 2 in done_after:
-                project(done_after[k - 2])
-            for i in norm_at.get(k - 1, []):
-                turn(*late[i])
-                group_unit(*late[i])
-            if k == 5:
+            for m in range(8):
+                if k == last_slot[m] + 2:
+                    project(m)
+            for m in range(3, 8):
+                j = k - (6 + 2 * (m - 3)) + 2
+                if j == 0:
+                    for c in range(CHUNKS):
+                        turn(m, c)
+                    new_values(m, 0, 2)
+                    new_values(m, 2, 2)
+            if k == 0:
+                turn(2, 3)
+                group_unit(2, 3)
+                quantise_h(0, 1)
+                quantise(2, 3, 1)
+                regroup_h(3, 1, vcopy)
+                quantise_h(2, 1)
+                quantise_h(3, 1)
+            if k == 1:
                 turn_w2(0)
                 turn_w2(1)
                 group_w2(0)
+            if k == 2:
                 group_w2(1)
-            if k == 5 + 2:
+            if k == 4:
                 quantise_w2()
-
-            if k - 1 in done_after:
-                quantise_agg(done_after[k - 1])
-            for i in norm_at.get(k, []):
-                normalise(*late[i])
-            for i in norm_at.get(k - 2, []):
-                quantise_unit(*late[i])
-            if k - 3 in done_after:
-                finish(done_after[k - 3])
+            for m in range(8):
+                if k == last_slot[m] + 4:
+                    finish(m)
+            for m in range(8):
+                if k == last_slot[m] + 1:
+                    quantise_agg(m)
+            for m in range(3, 8):
+                j = k - (6 + 2 * (m - 3)) + 2
+                if j == 0:
+                    group_unit(m, 0)
+                    group_unit(m, 1)
+                    group_unit(m, 2)
+                    group_unit(m, 3)
+                if j == 1:
+                    quantise(m, 0, 2)
+                    quantise(m, 2, 2)
+                if j == -2:
+                    normalise(2 * m, 0, CHUNKS)
+                if j == -2 + 1:
+                    normalise(2 * m + 1, 0, CHUNKS)

@@ -167,22 +167,23 @@ def tile_simplegcn_pb_kernel(tc, h, adj, W2, b2, out):
 
         folded_banks = {}
 
-        def fold(r):
-            folded = agg_psum.tile([P, SUM_WIDTH], F32, tag="agg")
-            for n in range(NODES // SUM_WIDTH):
+        def fold(r, width=SUM_WIDTH):
+            folded = agg_psum.tile([P, width], F32, tag="agg")
+            for n in range(NODES // width):
                 nc.tensor.matmul(
                     out=folded[:],
                     lhsT=ident_bf16[:],
-                    rhs=adj_rows[:, r, n * SUM_WIDTH : (n + 1) * SUM_WIDTH],
+                    rhs=adj_rows[:, r, n * width : (n + 1) * width],
                     start=(n == 0),
-                    stop=(n == NODES // SUM_WIDTH - 1),
+                    stop=(n == NODES // width - 1),
                 )
             folded_banks[r] = folded
 
         def reduce(r):
             unused_folded = small.tile([P, SUM_WIDTH], BF16)
+            width = folded_banks[r].shape[1]
             nc.scalar.activation(
-                out=unused_folded[:], in_=folded_banks[r][:], func=ACT.Copy, accum_out=deg[:, r, 0:1]
+                out=unused_folded[:, 0:width], in_=folded_banks[r][:], func=ACT.Copy, accum_out=deg[:, r, 0:1]
             )
 
         def invert(r0, n):
@@ -193,41 +194,43 @@ def tile_simplegcn_pb_kernel(tc, h, adj, W2, b2, out):
         spread_banks = {}
 
         def spread(r0, n):
-            bank = agg_psum.tile([P, PACK, P], F32, tag="agg")
-            for place in range(n):
-                r = r0 + place
-                nc.tensor.transpose(bank[:, place, :], d_col[:, r : r + 1].to_broadcast([P, P]), ident_f32[:])
-            spread_banks[r0] = bank
+            band = r0 // 4
+            if band not in spread_banks:
+                bank = out_psum.tile([P, 4, P], F32, tag="out")
+                spread_banks[band] = bank
+            for place in range(r0 % 4, r0 % 4 + n):
+                r = 4 * band + place
+                nc.tensor.transpose(spread_banks[band][:, place, :], d_col[:, r : r + 1].to_broadcast([P, P]), ident_f32[:])
 
         def keep_row(r0, n):
             nc.scalar.copy(
                 out=d_row[:, r0 * P : (r0 + n) * P],
-                in_=spread_banks[r0][:, 0:n, :].rearrange("p l n -> p (l n)"),
+                in_=spread_banks[r0 // 4][:, r0 % 4 : r0 % 4 + n, :].rearrange("p l n -> p (l n)"),
             )
 
         row_operands = {}
         unit_values = {}
         turned_banks = {}
 
-        def normalise(r, c, width):
+        def normalise(r, c, width, factors=None):
             cols = slice(c * K_PASS, (c + width) * K_PASS)
             nc.vector.scalar_tensor_tensor(
                 out=adj_rows[:, r, cols],
                 in0=adj_rows[:, r, cols],
                 scalar=d_col[:, r : r + 1],
-                in1=d_row[:, cols],
+                in1=d_row[:, cols] if factors is None else factors,
                 op0=ALU.mult,
                 op1=ALU.mult,
             )
 
-        def norm_unit(m, c):
-            normalise(2 * m, c, 1)
-            normalise(2 * m + 1, c, 1)
+        def norm_unit(m, c, factors=None):
+            normalise(2 * m, c, 1, factors)
+            normalise(2 * m + 1, c, 1, factors)
 
-        def turn(m, c):
+        def turn(m, c, places=(0, 1)):
             turned = turn_psum.tile([P, 2, 2, P], F32, tag="turn")
-            turned_banks[(m, c)] = turned
-            for place in range(2):
+            for place in places:
+                turned_banks[(m, c, place)] = turned
                 words = adj_rows[:, 2 * m + place, :].bitcast(F32)
                 for u in range(2):
                     w0 = c * (K_PASS // 2) + u * P
@@ -238,22 +241,36 @@ def tile_simplegcn_pb_kernel(tc, h, adj, W2, b2, out):
             for n in range(width):
                 unit_values[(m, c + n)] = (grouped, n)
 
-        def group_unit(m, c):
+        def group_unit(m, c, places=(0, 1)):
             if (m, c) not in unit_values:
                 new_values(m, c, 1)
             grouped, n = unit_values[(m, c)]
+            first, end = places[0], places[-1] + 1
             nc.scalar.copy(
-                out=grouped[:, n * 2 * K_PASS : (n + 1) * 2 * K_PASS]
+                out=grouped[:, (2 * n + first) * K_PASS : (2 * n + end) * K_PASS]
                 .bitcast(F32)
-                .rearrange("p (l i u) -> p l i u", l=2, u=2),
-                in_=turned_banks[(m, c)][:].rearrange("p l u i -> p l i u"),
+                .rearrange("p (l i u) -> p l i u", l=end - first, u=2),
+                in_=turned_banks[(m, c, first)][:, first:end, :, :].rearrange("p l u i -> p l i u"),
             )
 
-        def quantise(m, c, width):
+        def quantise_one(m, c, place):
+            operand(m)
+            a_codes, a_scales = row_operands[m]
+            cols = slice(place * P, (place + 1) * P)
+            nc.vector.quantize_mx(
+                out=a_codes[:, c, cols].bitcast(FP8X4),
+                scales=a_scales[:, c, cols],
+                in_=unit_values[(m, c)][0][:, place * K_PASS : (place + 1) * K_PASS],
+            )
+
+        def operand(m):
             if m not in row_operands:
                 a_codes = a_stage.tile([P, CHUNKS, 2 * P], U32, align_bytes=64)
                 a_scales = a_stage.tile([P, CHUNKS, 2 * P], U8, align_bytes=64)
                 row_operands[m] = (a_codes, a_scales)
+
+        def quantise(m, c, width):
+            operand(m)
             a_codes, a_scales = row_operands[m]
             nc.vector.quantize_mx(
                 out=a_codes[:, c : c + width, :].rearrange("p c i -> p (c i)").bitcast(FP8X4),
@@ -266,55 +283,57 @@ def tile_simplegcn_pb_kernel(tc, h, adj, W2, b2, out):
         g_operands = {}
         out_banks = {}
 
-        def aggregate(m, g):
-            if m not in g_values:
-                agg_grouped = g_stage.tile([P, F_PASSES, 2 * P, PACK], BF16, align_bytes=64)
-                g_values[m] = agg_grouped
-            a_codes, a_scales = row_operands[m]
-            for q in range(2):
-                agg_t = agg_psum.tile([P, 2, 2 * P], F32, tag="agg")
-                for s in range(2):
-                    f0 = g * K_PASS + (2 * q + s) * P
-                    for c in range(CHUNKS):
-                        nc.tensor.matmul_mx(
-                            out=agg_t[:, s, :],
-                            lhsT=h_codes[:, c, f0 : f0 + P].bitcast(FP8X4),
-                            lhsT_scale=h_scales[:, c, f0 : f0 + P],
-                            rhs=a_codes[:, c, :].bitcast(FP8X4),
-                            rhs_scale=a_scales[:, c, :],
-                            start=(c == 0),
-                            stop=(c == CHUNKS - 1),
-                        )
-                agg_banks[(m, g, q)] = agg_t
+        def aggregate(r, g):
+            a_codes, a_scales = row_operands[r // 2]
+            cols = slice((r % 2) * P, (r % 2 + 1) * P)
+            agg_t = agg_psum.tile([P, PACK, P], F32, tag="agg")
+            agg_banks[(r, g)] = agg_t
+            for t in range(PACK):
+                f0 = g * K_PASS + t * P
+                for c in range(CHUNKS):
+                    nc.tensor.matmul_mx(
+                        out=agg_t[:, t, :],
+                        lhsT=h_codes[:, c, f0 : f0 + P].bitcast(FP8X4),
+                        lhsT_scale=h_scales[:, c, f0 : f0 + P],
+                        rhs=a_codes[:, c, cols].bitcast(FP8X4),
+                        rhs_scale=a_scales[:, c, cols],
+                        start=(c == 0),
+                        stop=(c == CHUNKS - 1),
+                    )
 
-        def group_agg(m, g):
-            for q in range(2):
-                nc.scalar.copy(
-                    out=g_values[m][:, g, :, 2 * q : 2 * q + 2],
-                    in_=agg_banks[(m, g, q)][:].rearrange("p s i -> p i s"),
-                )
-
-        def quantise_agg(m):
-            agg_codes = g_stage.tile([P, F_PASSES, 2 * P], U32, align_bytes=64, bufs=2)
-            agg_scales = g_stage.tile([P, F_PASSES, 2 * P], U8, align_bytes=64, bufs=2)
-            g_operands[m] = (agg_codes, agg_scales)
-            nc.vector.quantize_mx(
-                out=agg_codes[:].rearrange("p g i -> p (g i)").bitcast(FP8X4),
-                scales=agg_scales[:].rearrange("p g i -> p (g i)"),
-                in_=g_values[m][:].rearrange("p g i t -> p (g i t)"),
+        def group_agg(r, g, copy=nc.scalar.copy):
+            if r // 2 not in g_values:
+                agg_grouped = g_stage.tile([P, 2, F_PASSES, P, PACK], BF16, align_bytes=64)
+                g_values[r // 2] = agg_grouped
+            copy(
+                out=g_values[r // 2][:, r % 2, g, :, :],
+                in_=agg_banks[(r, g)][:].rearrange("p t i -> p i t"),
             )
 
-        def project(m):
+        def quantise_agg(m, first=0, count=4):
+            if m not in g_operands:
+                agg_codes = g_stage.tile([P, 4, P], U32, align_bytes=64, bufs=2)
+                agg_scales = g_stage.tile([P, 4, P], U8, align_bytes=64, bufs=2)
+                g_operands[m] = (agg_codes, agg_scales)
             agg_codes, agg_scales = g_operands[m]
-            out_rows = out_psum.tile([P, 2, OUT], F32, tag="out")
-            out_banks[m] = out_rows
-            for place in range(2):
-                cols = slice(place * P, (place + 1) * P)
+            parts = slice(first, first + count)
+            nc.vector.quantize_mx(
+                out=agg_codes[:, parts, :].rearrange("p k i -> p (k i)").bitcast(FP8X4),
+                scales=agg_scales[:, parts, :].rearrange("p k i -> p (k i)"),
+                in_=g_values[m][:].rearrange("p l g i t -> p (l g) (i t)")[:, parts, :].rearrange("p k x -> p (k x)"),
+            )
+
+        def project(m, places=(0, 1)):
+            if m not in out_banks:
+                out_rows = out_psum.tile([P, 2, OUT], F32, tag="out")
+                out_banks[m] = out_rows
+            agg_codes, agg_scales = g_operands[m]
+            for place in places:
                 for g in range(F_PASSES):
                     nc.tensor.matmul_mx(
-                        out=out_rows[:, place, :],
-                        lhsT=agg_codes[:, g, cols].bitcast(FP8X4),
-                        lhsT_scale=agg_scales[:, g, cols],
+                        out=out_banks[m][:, place, :],
+                        lhsT=agg_codes[:, 2 * place + g, :].bitcast(FP8X4),
+                        lhsT_scale=agg_scales[:, 2 * place + g, :],
                         rhs=w2_codes[:, g, :].bitcast(FP8X4),
                         rhs_scale=w2_scales[:, g, :],
                         start=(g == 0),
@@ -327,6 +346,21 @@ def tile_simplegcn_pb_kernel(tc, h, adj, W2, b2, out):
             nc.sync.dma_start(
                 out=out[2 * m * P : 2 * (m + 1) * P, :].rearrange("(l p) o -> p l o", l=2), in_=result[:]
             )
+
+        def group_agg_half(r, g, half, copy):
+            rows = slice(half * (P // 2), (half + 1) * (P // 2))
+            copy(
+                out=g_values[r // 2][:, r % 2, g, rows, :],
+                in_=agg_banks[(r, g)][:, :, rows].rearrange("p t i -> p i t"),
+            )
+
+        def finish_place(m, place):
+            r = 2 * m + place
+            result = o_stage.tile([P, OUT], F32, tag="place")
+            nc.vector.tensor_tensor(
+                out=result[:], in0=out_banks[m][:, place, :], in1=bias_rows[:, place, :], op=ALU.add
+            )
+            nc.sync.dma_start(out=out[r * P : (r + 1) * P, :], in_=result[:])
 
         vcopy, scopy = nc.vector.tensor_copy, nc.scalar.copy
         on_vector = (0, 1)
@@ -345,7 +379,7 @@ def tile_simplegcn_pb_kernel(tc, h, adj, W2, b2, out):
             elif s in on_scalar:
                 sum_direct(s, False)
             else:
-                fold(s)
+                fold(s, 128 if s == 15 else SUM_WIDTH)
             if s in (4, 8, 12):
                 spread(s - 4, 4)
             if s == 15:
@@ -360,7 +394,6 @@ def tile_simplegcn_pb_kernel(tc, h, adj, W2, b2, out):
                 invert(12, 3)
             if s == 15:
                 invert(15, 1)
-                keep_row(12, 3)
             for c, g, pieces in piece_at.get(s, ()):
                 regroup_h(c, g, scopy, pieces)
             if s == 4:
@@ -377,82 +410,97 @@ def tile_simplegcn_pb_kernel(tc, h, adj, W2, b2, out):
             if s in hq_at:
                 quantise_h(hq_at[s], 0)
         spread(15, 1)
-        keep_row(15, 1)
+        last_factors = spread_banks[3][:].rearrange("p l n -> p (l n)")
         turn(2, 1)
         group_unit(2, 1)
         turn(0, 2)
         group_unit(0, 2)
         turn(1, 2)
-        norm_unit(0, 3)
-        turn(0, 3)
-        group_unit(0, 3)
-        group_unit(1, 2)
+        normalise(0, 3, 1, last_factors)
+        turn(0, 3, (0,))
         quantise(0, 2, 1)
-        norm_unit(1, 3)
-        quantise(0, 3, 1)
-        turn(2, 2)
-        turn(1, 3)
-        group_unit(1, 3)
-        group_unit(2, 2)
-        quantise(1, 2, 1)
+        normalise(1, 3, 1, last_factors)
+        group_unit(0, 3, (0,))
+        turn(0, 3, (1,))
+        quantise_one(0, 3, 0)
+        group_unit(0, 3, (1,))
+        group_unit(1, 2)
         quantise(2, 1, 1)
-        norm_unit(2, 3)
-        quantise(1, 3, 1)
+        quantise_one(0, 3, 1)
+        norm_unit(1, 3, last_factors)
+        quantise(1, 2, 1)
         regroup_h(0, 1, scopy, (0, 1))
-        quantise(2, 2, 1)
-        regroup_h(1, 1, vcopy)
-        regroup_h(0, 1, scopy, (2, 3))
-        quantise_h(1, 1)
-        regroup_h(2, 1, vcopy)
-        slots = [(m, g) for g in range(2) for m in range(3)] + [(m, g) for m in range(3, 8) for g in range(2)]
-        last_slot = {m: slots.index((m, 1)) for m in range(8)}
+        norm_unit(2, 3, last_factors)
+        slots = [(r, g) for g in range(2) for r in range(6)] + [(r, g) for r in range(6, 16) for g in range(2)]
+        last_slot = {m: slots.index((2 * m + 1, 1)) for m in range(8)}
         for k in range(len(slots) + 4):
             if k < len(slots):
                 aggregate(*slots[k])
-                group_agg(*slots[k])
-            for m in range(8):
-                if k == last_slot[m] + 2:
+                if k < len(slots) - 1:
+                    group_agg(*slots[k])
+            for m in range(7):
+                if k == last_slot[m] + 4:
+                    finish(m)
+            for m in range(7):
+                if k == last_slot[m] + 3:
                     project(m)
             for m in range(3, 8):
-                j = k - (6 + 2 * (m - 3)) + 2
-                if j == 0:
+                if k == 12 + 4 * (m - 3) - 5:
                     for c in range(CHUNKS):
                         turn(m, c)
                     new_values(m, 0, 2)
                     new_values(m, 2, 2)
             if k == 0:
+                turn(2, 2)
+                turn(1, 3)
+                group_unit(1, 3)
+                group_unit(2, 2)
+                quantise(1, 3, 1)
+                regroup_h(2, 1, vcopy)
+                quantise(2, 2, 1)
+                regroup_h(0, 1, scopy, (2, 3))
+                quantise_h(2, 1)
+            if k == 1:
                 turn(2, 3)
                 group_unit(2, 3)
+                regroup_h(1, 1, scopy, (0, 1))
                 quantise_h(0, 1)
                 quantise(2, 3, 1)
                 regroup_h(3, 1, vcopy)
-                quantise_h(2, 1)
+            if k == 2:
+                regroup_h(1, 1, scopy, (2, 3))
+                keep_row(12, 4)
                 quantise_h(3, 1)
-            if k == 1:
+            if k == 4:
+                quantise_h(1, 1)
                 turn_w2(0)
                 turn_w2(1)
                 group_w2(0)
-            if k == 2:
+            if k == 6:
                 group_w2(1)
-            if k == 4:
+            if k == 8:
                 quantise_w2()
-            for m in range(8):
-                if k == last_slot[m] + 4:
-                    finish(m)
-            for m in range(8):
+            for m in range(7):
                 if k == last_slot[m] + 1:
                     quantise_agg(m)
             for m in range(3, 8):
-                j = k - (6 + 2 * (m - 3)) + 2
-                if j == 0:
-                    group_unit(m, 0)
-                    group_unit(m, 1)
-                    group_unit(m, 2)
-                    group_unit(m, 3)
-                if j == 1:
-                    quantise(m, 0, 2)
-                    quantise(m, 2, 2)
-                if j == -2:
+                j = k - (12 + 4 * (m - 3)) + 5
+                if j in (0, 1):
+                    group_unit(m, 2 * j)
+                    group_unit(m, 2 * j + 1)
+                if j in (2, 2 + 1):
+                    quantise(m, 2 * (j - 2), 2)
+                if j == -4:
                     normalise(2 * m, 0, CHUNKS)
-                if j == -2 + 1:
+                if j == -4 + 2:
                     normalise(2 * m + 1, 0, CHUNKS)
+            if k == len(slots) - 1:
+                quantise_agg(7, 0, 2)
+                project(7, (0,))
+                group_agg_half(15, 1, 0, scopy)
+                group_agg_half(15, 1, 1, vcopy)
+                quantise_agg(7, 2, 1)
+                finish_place(7, 0)
+                quantise_agg(7, 3, 1)
+                project(7, (1,))
+                finish_place(7, 1)

@@ -77,7 +77,7 @@ def tile_simplegcn_pb_kernel(tc, h, adj, W2, b2, out):
                     in_=h[j0 : j0 + K_PASS // 2, cols].rearrange("(p e) f -> p e f", e=2),
                 )
 
-        h_after = {3: 2, 7: 3}
+        h_after = {}
         for c in range(CHUNKS):
             if c not in h_after.values() and c < 2:
                 load_h(c, 0)
@@ -363,15 +363,16 @@ def tile_simplegcn_pb_kernel(tc, h, adj, W2, b2, out):
             nc.sync.dma_start(out=out[r * P : (r + 1) * P, :], in_=result[:])
 
         vcopy, scopy = nc.vector.tensor_copy, nc.scalar.copy
-        on_vector = (0, 1)
+        on_vector = (1, 4)
         on_scalar = ()
-        norm_at = {5: (0, 0), 6: (1, 0), 9: (0, 1), 10: (1, 1), 11: (2, 0), 12: (2, 1), 13: (0, 2), 14: (1, 2), 15: (2, 2)}
-        turn_at = {7: (0, 0), 8: (1, 0), 11: (0, 1), 12: (1, 1), 14: (2, 0)}
-        quant_at = {8: (0, 0), 9: (1, 0), 12: (0, 1), 13: (1, 1), 15: (2, 0)}
+        norm_at = {4: ((0, 0), (1, 0)), 6: ((2, 0),), 7: ((3, 0),), 8: ((0, 1), (1, 1)), 10: ((2, 1),), 11: ((3, 1),), 12: ((0, 2),), 14: ((1, 2),)}
+        turn_at = {8: ((0, 0), (1, 0), (2, 0)), 12: ((3, 0), (0, 1), (1, 1), (2, 1))}
+        quant_at = {9: ((0, 0), (1, 0)), 10: ((2, 0),), 13: ((3, 0), (0, 1)), 14: ((1, 1),), 15: ((2, 1),)}
         piece_at = {}
-        hq_at = {2: 1, 5: 2, 9: 3}
+        hq_at = {1: 1}
+        inv_at = {3: (0, 4), 5: (4, 2), 7: (6, 2), 9: (8, 2), 11: (10, 2)}
         regroup_h(0, 0, scopy)
-        regroup_h(1, 0, scopy)
+        regroup_h(1, 0, vcopy)
         quantise_h(0, 0)
         for s in range(ROW_TILES):
             if s in on_vector:
@@ -382,55 +383,57 @@ def tile_simplegcn_pb_kernel(tc, h, adj, W2, b2, out):
                 fold(s, 128 if s == 15 else SUM_WIDTH)
             if s in (4, 8, 12):
                 spread(s - 4, 4)
+            for u in turn_at.get(s, ()):
+                turn(*u)
             if s == 15:
                 spread(12, 3)
             if s not in on_vector and s not in on_scalar:
                 reduce(s)
             if s in (4, 8, 12):
                 keep_row(s - 4, 4)
-            if s in (3, 7, 11):
-                invert(s - 3, 4)
+            for u in turn_at.get(s, ()):
+                group_unit(*u)
+            if s in inv_at:
+                invert(*inv_at[s])
             if s == 14:
                 invert(12, 3)
             if s == 15:
                 invert(15, 1)
             for c, g, pieces in piece_at.get(s, ()):
                 regroup_h(c, g, scopy, pieces)
-            if s == 4:
-                regroup_h(2, 0, vcopy)
-            if s == 8:
-                regroup_h(3, 0, vcopy)
-            if s in norm_at:
-                norm_unit(*norm_at[s])
-            if s in turn_at:
-                turn(*turn_at[s])
-                group_unit(*turn_at[s])
-            if s in quant_at:
-                quantise(*quant_at[s], 1)
+
+            for u in norm_at.get(s, ()):
+                norm_unit(*u)
+            for u in quant_at.get(s, ()):
+                quantise(*u, 1)
             if s in hq_at:
                 quantise_h(hq_at[s], 0)
         spread(15, 1)
         last_factors = spread_banks[3][:].rearrange("p l n -> p (l n)")
-        turn(2, 1)
-        group_unit(2, 1)
+        turn(3, 1)
         turn(0, 2)
+        regroup_h(3, 0, scopy, (0, 1))
         group_unit(0, 2)
-        turn(1, 2)
+        regroup_h(2, 0, vcopy)
         normalise(0, 3, 1, last_factors)
         turn(0, 3, (0,))
+        quantise_h(2, 0)
         quantise(0, 2, 1)
         normalise(1, 3, 1, last_factors)
         group_unit(0, 3, (0,))
         turn(0, 3, (1,))
         quantise_one(0, 3, 0)
+        regroup_h(3, 0, scopy, (2, 3))
         group_unit(0, 3, (1,))
-        group_unit(1, 2)
-        quantise(2, 1, 1)
+        group_unit(3, 1)
+        quantise_h(3, 0)
         quantise_one(0, 3, 1)
         norm_unit(1, 3, last_factors)
-        quantise(1, 2, 1)
+        quantise(3, 1, 1)
+        norm_unit(2, 2)
         regroup_h(0, 1, scopy, (0, 1))
         norm_unit(2, 3, last_factors)
+        late_from = {3: 2, 4: 0, 5: 0, 6: 0, 7: 0}
         slots = [(r, g) for g in range(2) for r in range(6)] + [(r, g) for r in range(6, 16) for g in range(2)]
         last_slot = {m: slots.index((2 * m + 1, 1)) for m in range(8)}
         for k in range(len(slots) + 4):
@@ -446,15 +449,18 @@ def tile_simplegcn_pb_kernel(tc, h, adj, W2, b2, out):
                     project(m)
             for m in range(3, 8):
                 if k == 12 + 4 * (m - 3) - 5:
-                    for c in range(CHUNKS):
+                    for c in range(late_from[m], CHUNKS):
                         turn(m, c)
-                    new_values(m, 0, 2)
-                    new_values(m, 2, 2)
+                    for c in range(late_from[m], CHUNKS, 2):
+                        new_values(m, c, 2)
             if k == 0:
-                turn(2, 2)
+                turn(1, 2)
                 turn(1, 3)
+                turn(2, 2)
+                group_unit(1, 2)
                 group_unit(1, 3)
                 group_unit(2, 2)
+                quantise(1, 2, 1)
                 quantise(1, 3, 1)
                 regroup_h(2, 1, vcopy)
                 quantise(2, 2, 1)
@@ -463,16 +469,16 @@ def tile_simplegcn_pb_kernel(tc, h, adj, W2, b2, out):
             if k == 1:
                 turn(2, 3)
                 group_unit(2, 3)
+                keep_row(12, 4)
                 regroup_h(1, 1, scopy, (0, 1))
                 quantise_h(0, 1)
                 quantise(2, 3, 1)
                 regroup_h(3, 1, vcopy)
             if k == 2:
                 regroup_h(1, 1, scopy, (2, 3))
-                keep_row(12, 4)
                 quantise_h(3, 1)
-            if k == 4:
                 quantise_h(1, 1)
+            if k == 4:
                 turn_w2(0)
                 turn_w2(1)
                 group_w2(0)
@@ -485,15 +491,15 @@ def tile_simplegcn_pb_kernel(tc, h, adj, W2, b2, out):
                     quantise_agg(m)
             for m in range(3, 8):
                 j = k - (12 + 4 * (m - 3)) + 5
-                if j in (0, 1):
+                if j in (0, 1) and 2 * j >= late_from[m]:
                     group_unit(m, 2 * j)
                     group_unit(m, 2 * j + 1)
-                if j in (2, 2 + 1):
+                if j in (2, 2 + 1) and 2 * (j - 2) >= late_from[m]:
                     quantise(m, 2 * (j - 2), 2)
                 if j == -4:
-                    normalise(2 * m, 0, CHUNKS)
+                    normalise(2 * m, late_from[m], CHUNKS - late_from[m])
                 if j == -4 + 2:
-                    normalise(2 * m + 1, 0, CHUNKS)
+                    normalise(2 * m + 1, late_from[m], CHUNKS - late_from[m])
             if k == len(slots) - 1:
                 quantise_agg(7, 0, 2)
                 project(7, (0,))

@@ -362,6 +362,28 @@ def tile_simplegcn_pb_kernel(tc, h, adj, W2, b2, out):
             )
             nc.sync.dma_start(out=out[r * P : (r + 1) * P, :], in_=result[:])
 
+        last_bank = {}
+
+        def project_last(g):
+            if g == 0:
+                last_rows = turn_psum.tile([P, OUT], F32, tag="turn")
+                last_bank[0] = last_rows
+            agg_codes, agg_scales = g_operands[7]
+            nc.tensor.matmul_mx(
+                out=last_bank[0][:],
+                lhsT=agg_codes[:, 2 + g, :].bitcast(FP8X4),
+                lhsT_scale=agg_scales[:, 2 + g, :],
+                rhs=w2_codes[:, g, :].bitcast(FP8X4),
+                rhs_scale=w2_scales[:, g, :],
+                start=(g == 0),
+                stop=(g == F_PASSES - 1),
+            )
+
+        def finish_last():
+            result = o_stage.tile([P, OUT], F32, tag="place")
+            nc.vector.tensor_tensor(out=result[:], in0=last_bank[0][:], in1=bias_rows[:, 0, :], op=ALU.add)
+            nc.sync.dma_start(out=out[NODES - P :, :], in_=result[:])
+
         vcopy, scopy = nc.vector.tensor_copy, nc.scalar.copy
         on_vector = (1, 4)
         on_scalar = ()
@@ -442,17 +464,17 @@ def tile_simplegcn_pb_kernel(tc, h, adj, W2, b2, out):
                 if k < len(slots) - 1:
                     group_agg(*slots[k])
             for m in range(7):
-                if k == last_slot[m] + 4:
+                if k == last_slot[m] + 3:
                     finish(m)
             for m in range(7):
-                if k == last_slot[m] + 3:
+                if k == last_slot[m] + 2:
                     project(m)
             for m in range(3, 8):
-                if k == 12 + 4 * (m - 3) - 5:
-                    for c in range(late_from[m], CHUNKS):
-                        turn(m, c)
-                    for c in range(late_from[m], CHUNKS, 2):
-                        new_values(m, c, 2)
+                c = 2 * (k - (12 + 4 * (m - 3)) + 5)
+                if c in (0, 2) and c >= late_from[m]:
+                    turn(m, c)
+                    turn(m, c + 1)
+                    new_values(m, c, 2)
             if k == 0:
                 turn(1, 2)
                 turn(1, 3)
@@ -500,13 +522,14 @@ def tile_simplegcn_pb_kernel(tc, h, adj, W2, b2, out):
                     normalise(2 * m, late_from[m], CHUNKS - late_from[m])
                 if j == -4 + 2:
                     normalise(2 * m + 1, late_from[m], CHUNKS - late_from[m])
-            if k == len(slots) - 1:
+            if k == len(slots) - 2:
                 quantise_agg(7, 0, 2)
                 project(7, (0,))
-                group_agg_half(15, 1, 0, scopy)
-                group_agg_half(15, 1, 1, vcopy)
                 quantise_agg(7, 2, 1)
                 finish_place(7, 0)
+            if k == len(slots) - 1:
+                last_rows = project_last(0)
+                group_agg(15, 1)
                 quantise_agg(7, 3, 1)
-                project(7, (1,))
-                finish_place(7, 1)
+                project_last(1)
+                finish_last()

@@ -384,6 +384,23 @@ def tile_simplegcn_pb_kernel(tc, h, adj, W2, b2, out):
             nc.vector.tensor_tensor(out=result[:], in0=last_bank[0][:], in1=bias_rows[:, 0, :], op=ALU.add)
             nc.sync.dma_start(out=out[NODES - P :, :], in_=result[:])
 
+        idle_banks = []
+
+        def keep_warm(passes):
+            if not idle_banks:
+                idle_bank = agg_psum.tile([P, K_PASS], F32, tag="agg")
+                idle_banks.append(idle_bank)
+            for n in range(passes):
+                nc.tensor.matmul_mx(
+                    out=idle_banks[0][:],
+                    lhsT=h_codes[:, 0, 0:P].bitcast(FP8X4),
+                    lhsT_scale=h_scales[:, 0, 0:P],
+                    rhs=h_codes[:, 0, 0:K_PASS].bitcast(FP8X4),
+                    rhs_scale=h_scales[:, 0, 0:K_PASS],
+                    start=True,
+                    stop=True,
+                )
+
         vcopy, scopy = nc.vector.tensor_copy, nc.scalar.copy
         on_vector = (1, 4)
         on_scalar = ()
@@ -434,22 +451,26 @@ def tile_simplegcn_pb_kernel(tc, h, adj, W2, b2, out):
         last_factors = spread_banks[3][:].rearrange("p l n -> p (l n)")
         turn(3, 1)
         turn(0, 2)
+        keep_warm(1)
         regroup_h(3, 0, scopy, (0, 1))
-        group_unit(0, 2)
         regroup_h(2, 0, vcopy)
         normalise(0, 3, 1, last_factors)
         turn(0, 3, (0,))
-        quantise_h(2, 0)
-        quantise(0, 2, 1)
+        keep_warm(1)
+        regroup_h(3, 0, scopy, (2,))
+        regroup_h(3, 0, vcopy, (3,))
         normalise(1, 3, 1, last_factors)
         group_unit(0, 3, (0,))
         turn(0, 3, (1,))
-        quantise_one(0, 3, 0)
-        regroup_h(3, 0, scopy, (2, 3))
-        group_unit(0, 3, (1,))
-        group_unit(3, 1)
+        keep_warm(3)
+        quantise_h(2, 0)
+        group_unit(0, 2)
         quantise_h(3, 0)
+        group_unit(0, 3, (1,))
+        quantise_one(0, 3, 0)
+        quantise(0, 2, 1)
         quantise_one(0, 3, 1)
+        group_unit(3, 1)
         norm_unit(1, 3, last_factors)
         quantise(3, 1, 1)
         norm_unit(2, 2)
@@ -478,23 +499,23 @@ def tile_simplegcn_pb_kernel(tc, h, adj, W2, b2, out):
             if k == 0:
                 turn(1, 2)
                 turn(1, 3)
-                turn(2, 2)
                 group_unit(1, 2)
                 group_unit(1, 3)
-                group_unit(2, 2)
                 quantise(1, 2, 1)
                 quantise(1, 3, 1)
                 regroup_h(2, 1, vcopy)
-                quantise(2, 2, 1)
                 regroup_h(0, 1, scopy, (2, 3))
                 quantise_h(2, 1)
             if k == 1:
+                turn(2, 2)
                 turn(2, 3)
+                group_unit(2, 2)
                 group_unit(2, 3)
                 keep_row(12, 4)
                 regroup_h(1, 1, scopy, (0, 1))
-                quantise_h(0, 1)
+                quantise(2, 2, 1)
                 quantise(2, 3, 1)
+                quantise_h(0, 1)
                 regroup_h(3, 1, vcopy)
             if k == 2:
                 regroup_h(1, 1, scopy, (2, 3))

@@ -56,8 +56,8 @@ def tile_simplegcn_pb_kernel(tc, h, adj, W2, b2, out):
         eps_col = keep.tile([P, 1], F32)
         d_col = keep.tile([P, ROW_TILES], F32)
         d_row = keep.tile([P, NODES], F32)
-        h_codes = keep.tile([P, CHUNKS, HID], U32, align_bytes=64)
-        h_scales = keep.tile([P, CHUNKS, HID], U8, align_bytes=64)
+        h_codes = keep.tile([P, CHUNKS, HID], U32, align_bytes=256)
+        h_scales = keep.tile([P, CHUNKS, HID], U8, align_bytes=256)
         w2_grouped = keep.tile([P, F_PASSES, OUT, PACK], BF16, align_bytes=64)
         w2_codes = keep.tile([P, F_PASSES, OUT], U32, align_bytes=64)
         w2_scales = keep.tile([P, F_PASSES, OUT], U8, align_bytes=64)
@@ -129,15 +129,11 @@ def tile_simplegcn_pb_kernel(tc, h, adj, W2, b2, out):
             if (c, g) not in h_values:
                 h_grouped = h_stage.tile([P, K_PASS, PACK], BF16, align_bytes=64)
                 h_values[(c, g)] = h_grouped
-            if len(pieces) == 4:
-                spans = [(0, K_PASS)]
-            else:
-                spans = [(q * P, (q + 1) * P) for q in pieces]
-            for f0, f1 in spans:
-                copy(
-                    out=h_values[(c, g)][:, f0:f1, :].rearrange("p (a i) t -> p a t i", i=4),
-                    in_=h_rows[g][:, c, :, f0:f1].rearrange("p t (a i) -> p a t i", i=4),
-                )
+            cols = slice(pieces[0] * P, (pieces[-1] + 1) * P)
+            copy(
+                out=h_values[(c, g)][:, cols, :].rearrange("p (a i) t -> p a t i", i=4),
+                in_=h_rows[g][:, c, :, cols].rearrange("p t (a i) -> p a t i", i=4),
+            )
 
         def quantise_h(c, g):
             cols = slice(g * K_PASS, (g + 1) * K_PASS)
@@ -149,7 +145,7 @@ def tile_simplegcn_pb_kernel(tc, h, adj, W2, b2, out):
 
         def sum_direct(r, on_vector):
             if on_vector:
-                unused_vector = small.tile([P, NODES], BF16)
+                unused_vector = small.tile([P, NODES], BF16, bufs=1)
                 nc.vector.tensor_scalar(
                     out=unused_vector[:],
                     in0=adj_rows[:, r, :],
@@ -265,8 +261,8 @@ def tile_simplegcn_pb_kernel(tc, h, adj, W2, b2, out):
 
         def operand(m):
             if m not in row_operands:
-                a_codes = a_stage.tile([P, CHUNKS, 2 * P], U32, align_bytes=64)
-                a_scales = a_stage.tile([P, CHUNKS, 2 * P], U8, align_bytes=64)
+                a_codes = a_stage.tile([P, CHUNKS, 2 * P], U32, align_bytes=256)
+                a_scales = a_stage.tile([P, CHUNKS, 2 * P], U8, align_bytes=256)
                 row_operands[m] = (a_codes, a_scales)
 
         def quantise(m, c, width):
@@ -419,7 +415,7 @@ def tile_simplegcn_pb_kernel(tc, h, adj, W2, b2, out):
             elif s in on_scalar:
                 sum_direct(s, False)
             else:
-                fold(s, 128 if s == 15 else SUM_WIDTH)
+                fold(s, 128 if s == 15 else (SUM_WIDTH if s < 16 else 256))
             if s in (4, 8, 12):
                 spread(s - 4, 4)
             for u in turn_at.get(s, ()):

@@ -56,8 +56,8 @@ def tile_simplegcn_pb_kernel(tc, h, adj, W2, b2, out):
         eps_col = keep.tile([P, 1], F32)
         d_col = keep.tile([P, ROW_TILES], F32)
         d_row = keep.tile([P, NODES], F32)
-        h_codes = keep.tile([P, CHUNKS, HID], U32, align_bytes=256)
-        h_scales = keep.tile([P, CHUNKS, HID], U8, align_bytes=256)
+        h_codes = keep.tile([P, CHUNKS, HID], U32, align_bytes=64)
+        h_scales = keep.tile([P, CHUNKS, HID], U8, align_bytes=64)
         w2_grouped = keep.tile([P, F_PASSES, OUT, PACK], BF16, align_bytes=64)
         w2_codes = keep.tile([P, F_PASSES, OUT], U32, align_bytes=64)
         w2_scales = keep.tile([P, F_PASSES, OUT], U8, align_bytes=64)
@@ -77,9 +77,9 @@ def tile_simplegcn_pb_kernel(tc, h, adj, W2, b2, out):
                     in_=h[j0 : j0 + K_PASS // 2, cols].rearrange("(p e) f -> p e f", e=2),
                 )
 
-        h_after = {}
+        h_after = {3: 0, 7: 1}
         for c in range(CHUNKS):
-            if c not in h_after.values() and c < 2:
+            if c not in h_after.values() and c < 0:
                 load_h(c, 0)
         for r in range(ROW_TILES - 1):
             nc.sync.dma_start(out=adj_rows[:, r, :], in_=adj[r * P : (r + 1) * P, :])
@@ -88,7 +88,7 @@ def tile_simplegcn_pb_kernel(tc, h, adj, W2, b2, out):
         for half in range(2):
             cols = slice(half * NODES // 2, (half + 1) * NODES // 2)
             nc.sync.dma_start(out=adj_rows[:, ROW_TILES - 1, cols], in_=adj[NODES - P :, cols])
-        for c in range(2, CHUNKS):
+        for c in range(0, CHUNKS):
             if c not in h_after.values():
                 load_h(c, 0)
         for c in range(CHUNKS):
@@ -261,8 +261,8 @@ def tile_simplegcn_pb_kernel(tc, h, adj, W2, b2, out):
 
         def operand(m):
             if m not in row_operands:
-                a_codes = a_stage.tile([P, CHUNKS, 2 * P], U32, align_bytes=256)
-                a_scales = a_stage.tile([P, CHUNKS, 2 * P], U8, align_bytes=256)
+                a_codes = a_stage.tile([P, CHUNKS, 2 * P], U32, align_bytes=64)
+                a_scales = a_stage.tile([P, CHUNKS, 2 * P], U8, align_bytes=64)
                 row_operands[m] = (a_codes, a_scales)
 
         def quantise(m, c, width):
@@ -398,17 +398,15 @@ def tile_simplegcn_pb_kernel(tc, h, adj, W2, b2, out):
                 )
 
         vcopy, scopy = nc.vector.tensor_copy, nc.scalar.copy
-        on_vector = (1, 4)
+        on_vector = (0, 1)
         on_scalar = ()
         norm_at = {4: ((0, 0), (1, 0)), 6: ((2, 0),), 7: ((3, 0),), 8: ((0, 1), (1, 1)), 10: ((2, 1),), 11: ((3, 1),), 12: ((0, 2),), 14: ((1, 2),)}
         turn_at = {8: ((0, 0), (1, 0), (2, 0)), 12: ((3, 0), (0, 1), (1, 1), (2, 1))}
         quant_at = {9: ((0, 0), (1, 0)), 10: ((2, 0),), 13: ((3, 0), (0, 1)), 14: ((1, 1),), 15: ((2, 1),)}
         piece_at = {}
-        hq_at = {1: 1}
+        hq_at = {}
         inv_at = {3: (0, 4), 5: (4, 2), 7: (6, 2), 9: (8, 2), 11: (10, 2)}
-        regroup_h(0, 0, scopy)
-        regroup_h(1, 0, vcopy)
-        quantise_h(0, 0)
+        first = 0
         for s in range(ROW_TILES):
             if s in on_vector:
                 sum_direct(s, True)
@@ -436,7 +434,13 @@ def tile_simplegcn_pb_kernel(tc, h, adj, W2, b2, out):
                 invert(15, 1)
             for c, g, pieces in piece_at.get(s, ()):
                 regroup_h(c, g, scopy, pieces)
-
+            if s == 4:
+                regroup_h(0, 0, vcopy)
+                quantise_h(0, 0)
+            if s == 7:
+                regroup_h(1, 0, vcopy)
+            if s == 8:
+                quantise_h(1, 0)
             for u in norm_at.get(s, ()):
                 norm_unit(*u)
             for u in quant_at.get(s, ()):
@@ -487,11 +491,11 @@ def tile_simplegcn_pb_kernel(tc, h, adj, W2, b2, out):
                 if k == last_slot[m] + 2:
                     project(m)
             for m in range(3, 8):
-                c = 2 * (k - (12 + 4 * (m - 3)) + 5)
-                if c in (0, 2) and c >= late_from[m]:
-                    turn(m, c)
-                    turn(m, c + 1)
-                    new_values(m, c, 2)
+                if k == 12 + 4 * (m - 3) - 5:
+                    for c in range(late_from[m], CHUNKS):
+                        turn(m, c)
+                    for c in range(late_from[m], CHUNKS, 2):
+                        new_values(m, c, 2)
             if k == 0:
                 turn(1, 2)
                 turn(1, 3)

from contextlib import ExitStack

import concourse.mybir as mybir
from concourse.masks import make_identity

F32 = mybir.dt.float32
BF16 = mybir.dt.bfloat16
U32 = mybir.dt.uint32
U8 = mybir.dt.uint8
FP8X4 = mybir.dt.float8_e4m3fn_x4
ALU = mybir.AluOpType
ACT = mybir.ActivationFunctionType

P = 128
PACK = 4
K_PASS = P * PACK

NODES = 2048
HID = 1024
OUT = 256
EPS = 1e-8

ROW_TILES = NODES // P
CHUNKS = NODES // K_PASS
F_PASSES = HID // K_PASS
O_TILES = OUT // P
SUM_WIDTH = 512

FLOPS = 2 * NODES * NODES * HID + 2 * NODES * HID * OUT


def tile_simplegcn_pb_kernel(tc, h, adj, W2, b2, out):
    nc = tc.nc
    with ExitStack() as stack:
        keep = stack.enter_context(tc.tile_pool(name="keep", bufs=1))
        small = stack.enter_context(tc.tile_pool(name="small", bufs=2))
        h_stage = stack.enter_context(tc.tile_pool(name="h_stage", bufs=5))
        u_stage = stack.enter_context(tc.tile_pool(name="u_stage", bufs=4))
        a_stage = stack.enter_context(tc.tile_pool(name="a_stage", bufs=5))
        g_stage = stack.enter_context(tc.tile_pool(name="g_stage", bufs=4))
        o_stage = stack.enter_context(tc.tile_pool(name="o_stage", bufs=2))
        turn_psum = stack.enter_context(tc.psum_pool(name="turn_psum", bufs=4))
        agg_psum = stack.enter_context(tc.psum_pool(name="agg_psum", bufs=3))
        out_psum = stack.enter_context(tc.psum_pool(name="out_psum", bufs=1))
        stack.enter_context(tc.manual_schedule())

        ident_f32 = keep.tile([P, P], F32)
        ident_bf16 = keep.tile([P, P], BF16)
        w2_rows = keep.tile([P, O_TILES, HID], BF16)
        h_rows_0 = keep.tile([P, CHUNKS, PACK, K_PASS], BF16)
        h_rows_1 = keep.tile([P, CHUNKS, PACK, K_PASS], BF16)
        h_rows = (h_rows_0, h_rows_1)
        adj_rows = keep.tile([P, ROW_TILES, NODES], BF16)
        bias_rows = keep.tile([P, 2, OUT], BF16)
        deg = keep.tile([P, ROW_TILES, 8], F32)
        eps_col = keep.tile([P, 1], F32)
        d_col = keep.tile([P, ROW_TILES], F32)
        d_row = keep.tile([P, NODES], F32)
        h_codes = keep.tile([P, CHUNKS, HID], U32, align_bytes=64)
        h_scales = keep.tile([P, CHUNKS, HID], U8, align_bytes=64)
        w2_grouped = keep.tile([P, F_PASSES, OUT, PACK], BF16, align_bytes=64)
        w2_codes = keep.tile([P, F_PASSES, OUT], U32, align_bytes=64)
        w2_scales = keep.tile([P, F_PASSES, OUT], U8, align_bytes=64)

        nc.gpsimd.memset(eps_col[:], EPS)
        first_root = keep.tile([P, 1], F32)
        nc.scalar.activation(out=first_root[:], in_=eps_col[:], func=ACT.Abs_reciprocal_sqrt)
        make_identity(nc, ident_bf16[:])
        make_identity(nc, ident_f32[:])

        def load_h(c, g):
            cols = slice(g * K_PASS, (g + 1) * K_PASS)
            for u in range(2):
                j0 = c * K_PASS + u * (K_PASS // 2)
                nc.sync.dma_start(
                    out=h_rows[g][:, c, 2 * u : 2 * u + 2, :],
                    in_=h[j0 : j0 + K_PASS // 2, cols].rearrange("(p e) f -> p e f", e=2),
                )

        h_after = {3: 0, 7: 1}
        for c in range(CHUNKS):
            if c not in h_after.values() and c < 0:
                load_h(c, 0)
        for r in range(ROW_TILES - 1):
            nc.sync.dma_start(out=adj_rows[:, r, :], in_=adj[r * P : (r + 1) * P, :])
            if r in h_after:
                load_h(h_after[r], 0)
        for half in range(2):
            cols = slice(half * NODES // 2, (half + 1) * NODES // 2)
            nc.sync.dma_start(out=adj_rows[:, ROW_TILES - 1, cols], in_=adj[NODES - P :, cols])
        for c in range(0, CHUNKS):
            if c not in h_after.values():
                load_h(c, 0)
        for c in range(CHUNKS):
            load_h(c, 1)
        nc.sync.dma_start(out=w2_rows[:], in_=W2.rearrange("(b p) f -> p b f", p=P))
        nc.sync.dma_start(out=bias_rows[:, 0, :], in_=b2.partition_broadcast(P))
        nc.gpsimd.tensor_copy(out=bias_rows[:, 1, :], in_=bias_rows[:, 0, :])

        w2_banks = {}

        def turn_w2(g):
            w2_turned = turn_psum.tile([P, O_TILES, PACK, P], BF16, tag="turn")
            for b in range(O_TILES):
                for t in range(PACK):
                    f0 = g * K_PASS + t * P
                    nc.tensor.transpose(w2_turned[:, b, t, :], w2_rows[:, b, f0 : f0 + P], ident_bf16[:])
            w2_banks[g] = w2_turned

        def group_w2(g):
            nc.scalar.copy(
                out=w2_grouped[:, g, :, :].rearrange("p (b o) t -> p b o t", b=O_TILES),
                in_=w2_banks[g][:].rearrange("p b t o -> p b o t"),
            )

        def quantise_w2():
            nc.vector.quantize_mx(
                out=w2_codes[:].rearrange("p g o -> p (g o)").bitcast(FP8X4),
                scales=w2_scales[:].rearrange("p g o -> p (g o)"),
                in_=w2_grouped[:].rearrange("p g o t -> p (g o t)"),
            )

        h_values = {}

        def gcopy(out, in_):
            nc.gpsimd.tensor_scalar(out=out, in0=in_, scalar1=1.0, scalar2=0.0, op0=ALU.mult, op1=ALU.add)

        def regroup_h(c, g, copy, pieces=(0, 1, 2, 3)):
            if (c, g) not in h_values:
                h_grouped = h_stage.tile([P, K_PASS, PACK], BF16, align_bytes=64)
                h_values[(c, g)] = h_grouped
            cols = slice(pieces[0] * P, (pieces[-1] + 1) * P)
            copy(
                out=h_values[(c, g)][:, cols, :].rearrange("p (a i) t -> p a t i", i=4),
                in_=h_rows[g][:, c, :, cols].rearrange("p t (a i) -> p a t i", i=4),
            )

        def quantise_h(c, g):
            cols = slice(g * K_PASS, (g + 1) * K_PASS)
            nc.vector.quantize_mx(
                out=h_codes[:, c, cols].bitcast(FP8X4),
                scales=h_scales[:, c, cols],
                in_=h_values[(c, g)][:].rearrange("p f t -> p (f t)"),
            )

        def sum_direct(r, on_vector):
            if on_vector:
                unused_vector = small.tile([P, NODES], BF16, bufs=1)
                nc.vector.tensor_scalar(
                    out=unused_vector[:],
                    in0=adj_rows[:, r, :],
                    scalar1=1.0,
                    scalar2=None,
                    op0=ALU.mult,
                    op1=ALU.add,
                    accum_out=deg[:, r, 0:1],
                )
            else:
                unused_scalar = small.tile([P, NODES], BF16)
                nc.scalar.activation(
                    out=unused_scalar[:], in_=adj_rows[:, r, :], func=ACT.Copy, accum_out=deg[:, r, 0:1]
                )

        folded_banks = {}

        def fold(r, width=SUM_WIDTH):
            folded = agg_psum.tile([P, width], F32, tag="agg")
            for n in range(NODES // width):
                nc.tensor.matmul(
                    out=folded[:],
                    lhsT=ident_bf16[:],
                    rhs=adj_rows[:, r, n * width : (n + 1) * width],
                    start=(n == 0),
                    stop=(n == NODES // width - 1),
                )
            folded_banks[r] = folded

        def reduce(r):
            unused_folded = small.tile([P, SUM_WIDTH], BF16)
            width = folded_banks[r].shape[1]
            nc.scalar.activation(
                out=unused_folded[:, 0:width], in_=folded_banks[r][:], func=ACT.Copy, accum_out=deg[:, r, 0:1]
            )

        def invert(r0, n):
            nc.scalar.activation(
                out=d_col[:, r0 : r0 + n], in_=deg[:, r0 : r0 + n, 0], func=ACT.Abs_reciprocal_sqrt, bias=eps_col[:]
            )

        spread_banks = {}

        def spread(r0, n):
            band = r0 // 4
            if band not in spread_banks:
                bank = out_psum.tile([P, 4, P], F32, tag="out")
                spread_banks[band] = bank
            for place in range(r0 % 4, r0 % 4 + n):
                r = 4 * band + place
                nc.tensor.transpose(spread_banks[band][:, place, :], d_col[:, r : r + 1].to_broadcast([P, P]), ident_f32[:])

        def keep_row(r0, n):
            nc.scalar.copy(
                out=d_row[:, r0 * P : (r0 + n) * P],
                in_=spread_banks[r0 // 4][:, r0 % 4 : r0 % 4 + n, :].rearrange("p l n -> p (l n)"),
            )

        row_operands = {}
        unit_values = {}
        turned_banks = {}

        def normalise(r, c, width, factors=None):
            cols = slice(c * K_PASS, (c + width) * K_PASS)
            nc.vector.scalar_tensor_tensor(
                out=adj_rows[:, r, cols],
                in0=adj_rows[:, r, cols],
                scalar=d_col[:, r : r + 1],
                in1=d_row[:, cols] if factors is None else factors,
                op0=ALU.mult,
                op1=ALU.mult,
            )

        def norm_unit(m, c, factors=None):
            normalise(2 * m, c, 1, factors)
            normalise(2 * m + 1, c, 1, factors)

        def turn(m, c, places=(0, 1)):
            turned = turn_psum.tile([P, 2, 2, P], F32, tag="turn")
            for place in places:
                turned_banks[(m, c, place)] = turned
                words = adj_rows[:, 2 * m + place, :].bitcast(F32)
                for u in range(2):
                    w0 = c * (K_PASS // 2) + u * P
                    nc.tensor.transpose(turned[:, place, u, :], words[:, w0 : w0 + P], ident_f32[:])

        def new_values(m, c, width):
            grouped = u_stage.tile([P, width * 2 * K_PASS], BF16, align_bytes=64, tag="grouped_%d" % width, bufs=width == 1 and 4 or 3)
            for n in range(width):
                unit_values[(m, c + n)] = (grouped, n)

        def group_unit(m, c, places=(0, 1)):
            if (m, c) not in unit_values:
                new_values(m, c, 1)
            grouped, n = unit_values[(m, c)]
            first, end = places[0], places[-1] + 1
            nc.scalar.copy(
                out=grouped[:, (2 * n + first) * K_PASS : (2 * n + end) * K_PASS]
                .bitcast(F32)
                .rearrange("p (l i u) -> p l i u", l=end - first, u=2),
                in_=turned_banks[(m, c, first)][:, first:end, :, :].rearrange("p l u i -> p l i u"),
            )

        def quantise_one(m, c, place):
            operand(m)
            a_codes, a_scales = row_operands[m]
            cols = slice(place * P, (place + 1) * P)
            nc.vector.quantize_mx(
                out=a_codes[:, c, cols].bitcast(FP8X4),
                scales=a_scales[:, c, cols],
                in_=unit_values[(m, c)][0][:, place * K_PASS : (place + 1) * K_PASS],
            )

        def operand(m):
            if m not in row_operands:
                a_codes = a_stage.tile([P, CHUNKS, 2 * P], U32, align_bytes=64)
                a_scales = a_stage.tile([P, CHUNKS, 2 * P], U8, align_bytes=64)
                row_operands[m] = (a_codes, a_scales)

        def quantise(m, c, width):
            operand(m)
            a_codes, a_scales = row_operands[m]
            nc.vector.quantize_mx(
                out=a_codes[:, c : c + width, :].rearrange("p c i -> p (c i)").bitcast(FP8X4),
                scales=a_scales[:, c : c + width, :].rearrange("p c i -> p (c i)"),
                in_=unit_values[(m, c)][0][:],
            )

        agg_banks = {}
        g_values = {}
        g_operands = {}
        out_banks = {}

        def aggregate(r, g):
            a_codes, a_scales = row_operands[r // 2]
            cols = slice((r % 2) * P, (r % 2 + 1) * P)
            agg_t = agg_psum.tile([P, PACK, P], F32, tag="agg")
            agg_banks[(r, g)] = agg_t
            for t in range(PACK):
                f0 = g * K_PASS + t * P
                for c in range(CHUNKS):
                    nc.tensor.matmul_mx(
                        out=agg_t[:, t, :],
                        lhsT=h_codes[:, c, f0 : f0 + P].bitcast(FP8X4),
                        lhsT_scale=h_scales[:, c, f0 : f0 + P],
                        rhs=a_codes[:, c, cols].bitcast(FP8X4),
                        rhs_scale=a_scales[:, c, cols],
                        start=(c == 0),
                        stop=(c == CHUNKS - 1),
                    )

        def group_agg(r, g, copy=nc.scalar.copy):
            if r // 2 not in g_values:
                agg_grouped = g_stage.tile([P, 2, F_PASSES, P, PACK], BF16, align_bytes=64)
                g_values[r // 2] = agg_grouped
            copy(
                out=g_values[r // 2][:, r % 2, g, :, :],
                in_=agg_banks[(r, g)][:].rearrange("p t i -> p i t"),
            )

        def quantise_agg(m, first=0, count=4):
            if m not in g_operands:
                agg_codes = g_stage.tile([P, 4, P], U32, align_bytes=64, bufs=2)
                agg_scales = g_stage.tile([P, 4, P], U8, align_bytes=64, bufs=2)
                g_operands[m] = (agg_codes, agg_scales)
            agg_codes, agg_scales = g_operands[m]
            parts = slice(first, first + count)
            nc.vector.quantize_mx(
                out=agg_codes[:, parts, :].rearrange("p k i -> p (k i)").bitcast(FP8X4),
                scales=agg_scales[:, parts, :].rearrange("p k i -> p (k i)"),
                in_=g_values[m][:].rearrange("p l g i t -> p (l g) (i t)")[:, parts, :].rearrange("p k x -> p (k x)"),
            )

        def project(m, places=(0, 1)):
            if m not in out_banks:
                out_rows = out_psum.tile([P, 2, OUT], F32, tag="out")
                out_banks[m] = out_rows
            agg_codes, agg_scales = g_operands[m]
            for place in places:
                for g in range(F_PASSES):
                    nc.tensor.matmul_mx(
                        out=out_banks[m][:, place, :],
                        lhsT=agg_codes[:, 2 * place + g, :].bitcast(FP8X4),
                        lhsT_scale=agg_scales[:, 2 * place + g, :],
                        rhs=w2_codes[:, g, :].bitcast(FP8X4),
                        rhs_scale=w2_scales[:, g, :],
                        start=(g == 0),
                        stop=(g == F_PASSES - 1),
                    )

        def finish(m):
            result = o_stage.tile([P, 2, OUT], F32)
            nc.vector.tensor_tensor(out=result[:], in0=out_banks[m][:], in1=bias_rows[:], op=ALU.add)
            nc.sync.dma_start(
                out=out[2 * m * P : 2 * (m + 1) * P, :].rearrange("(l p) o -> p l o", l=2), in_=result[:]
            )

        def group_agg_half(r, g, half, copy):
            rows = slice(half * (P // 2), (half + 1) * (P // 2))
            copy(
                out=g_values[r // 2][:, r % 2, g, rows, :],
                in_=agg_banks[(r, g)][:, :, rows].rearrange("p t i -> p i t"),
            )

        def finish_place(m, place):
            r = 2 * m + place
            result = o_stage.tile([P, OUT], F32, tag="place")
            nc.vector.tensor_tensor(
                out=result[:], in0=out_banks[m][:, place, :], in1=bias_rows[:, place, :], op=ALU.add
            )
            nc.sync.dma_start(out=out[r * P : (r + 1) * P, :], in_=result[:])

        last_bank = {}

        def project_last(g):
            if g == 0:
                last_rows = turn_psum.tile([P, OUT], F32, tag="turn")
                last_bank[0] = last_rows
            agg_codes, agg_scales = g_operands[7]
            nc.tensor.matmul_mx(
                out=last_bank[0][:],
                lhsT=agg_codes[:, 2 + g, :].bitcast(FP8X4),
                lhsT_scale=agg_scales[:, 2 + g, :],
                rhs=w2_codes[:, g, :].bitcast(FP8X4),
                rhs_scale=w2_scales[:, g, :],
                start=(g == 0),
                stop=(g == F_PASSES - 1),
            )

        def finish_last():
            result = o_stage.tile([P, OUT], F32, tag="place")
            nc.vector.tensor_tensor(out=result[:], in0=last_bank[0][:], in1=bias_rows[:, 0, :], op=ALU.add)
            nc.sync.dma_start(out=out[NODES - P :, :], in_=result[:])

        idle_banks = []

        def keep_warm(passes):
            if not idle_banks:
                idle_bank = agg_psum.tile([P, K_PASS], F32, tag="agg")
                idle_banks.append(idle_bank)
            for n in range(passes):
                nc.tensor.matmul_mx(
                    out=idle_banks[0][:],
                    lhsT=h_codes[:, 0, 0:P].bitcast(FP8X4),
                    lhsT_scale=h_scales[:, 0, 0:P],
                    rhs=h_codes[:, 0, 0:K_PASS].bitcast(FP8X4),
                    rhs_scale=h_scales[:, 0, 0:K_PASS],
                    start=True,
                    stop=True,
                )

        vcopy, scopy = nc.vector.tensor_copy, nc.scalar.copy
        on_vector = (0, 1)
        on_scalar = ()
        norm_at = {4: ((0, 0), (1, 0)), 6: ((2, 0),), 7: ((3, 0),), 8: ((0, 1), (1, 1)), 10: ((2, 1),), 11: ((3, 1),), 12: ((0, 2),), 14: ((1, 2),)}
        turn_at = {8: ((0, 0), (1, 0), (2, 0)), 12: ((3, 0), (0, 1), (1, 1), (2, 1))}
        quant_at = {9: ((0, 0), (1, 0)), 10: ((2, 0),), 13: ((3, 0), (0, 1)), 14: ((1, 1),), 15: ((2, 1),)}
        piece_at = {}
        hq_at = {}
        inv_at = {3: (0, 4), 5: (4, 2), 7: (6, 2), 9: (8, 2), 11: (10, 2)}
        first = 0
        for s in range(ROW_TILES):
            if s in on_vector:
                sum_direct(s, True)
            elif s in on_scalar:
                sum_direct(s, False)
            else:
                fold(s, 128 if s == 15 else (SUM_WIDTH if s < 16 else 256))
            if s in (4, 8, 12):
                spread(s - 4, 4)
            for u in turn_at.get(s, ()):
                turn(*u)
            if s == 15:
                spread(12, 3)
            if s not in on_vector and s not in on_scalar:
                reduce(s)
            if s in (4, 8, 12):
                keep_row(s - 4, 4)
            for u in turn_at.get(s, ()):
                group_unit(*u)
            if s in inv_at:
                invert(*inv_at[s])
            if s == 14:
                invert(12, 3)
            if s == 15:
                invert(15, 1)
            for c, g, pieces in piece_at.get(s, ()):
                regroup_h(c, g, scopy, pieces)
            if s == 4:
                regroup_h(0, 0, vcopy)
                quantise_h(0, 0)
            if s == 7:
                regroup_h(1, 0, vcopy)
            if s == 8:
                quantise_h(1, 0)
            for u in norm_at.get(s, ()):
                norm_unit(*u)
            for u in quant_at.get(s, ()):
                quantise(*u, 1)
            if s in hq_at:
                quantise_h(hq_at[s], 0)
        spread(15, 1)
        last_factors = spread_banks[3][:].rearrange("p l n -> p (l n)")
        turn(3, 1)
        turn(0, 2)
        keep_warm(1)
        regroup_h(3, 0, scopy, (0, 1))
        regroup_h(2, 0, vcopy)
        normalise(0, 3, 1, last_factors)
        turn(0, 3, (0,))
        keep_warm(1)
        regroup_h(3, 0, scopy, (2,))
        regroup_h(3, 0, vcopy, (3,))
        normalise(1, 3, 1, last_factors)
        group_unit(0, 3, (0,))
        turn(0, 3, (1,))
        keep_warm(3)
        quantise_h(2, 0)
        group_unit(0, 2)
        quantise_h(3, 0)
        group_unit(0, 3, (1,))
        quantise_one(0, 3, 0)
        quantise(0, 2, 1)
        quantise_one(0, 3, 1)
        group_unit(3, 1)
        norm_unit(1, 3, last_factors)
        quantise(3, 1, 1)
        norm_unit(2, 2)
        regroup_h(0, 1, scopy, (0, 1))
        norm_unit(2, 3, last_factors)
        late_from = {3: 2, 4: 0, 5: 0, 6: 0, 7: 0}
        slots = [(r, g) for g in range(2) for r in range(6)] + [(r, g) for r in range(6, 16) for g in range(2)]
        last_slot = {m: slots.index((2 * m + 1, 1)) for m in range(8)}
        for k in range(len(slots) + 4):
            if k < len(slots):
                aggregate(*slots[k])
                if k < len(slots) - 1:
                    group_agg(*slots[k])
            for m in range(7):
                if k == last_slot[m] + 3:
                    finish(m)
            for m in range(7):
                if k == last_slot[m] + 2:
                    project(m)
            for m in range(3, 8):
                if k == 12 + 4 * (m - 3) - 5:
                    for c in range(late_from[m], CHUNKS):
                        turn(m, c)
                    for c in range(late_from[m], CHUNKS, 2):
                        new_values(m, c, 2)
            if k == 0:
                turn(1, 2)
                turn(1, 3)
                group_unit(1, 2)
                group_unit(1, 3)
                quantise(1, 2, 1)
                quantise(1, 3, 1)
                regroup_h(2, 1, vcopy)
                regroup_h(0, 1, scopy, (2, 3))
                quantise_h(2, 1)
            if k == 1:
                turn(2, 2)
                turn(2, 3)
                group_unit(2, 2)
                group_unit(2, 3)
                keep_row(12, 4)
                regroup_h(1, 1, scopy, (0, 1))
                quantise(2, 2, 1)
                quantise(2, 3, 1)
                quantise_h(0, 1)
                regroup_h(3, 1, vcopy)
            if k == 2:
                regroup_h(1, 1, scopy, (2, 3))
                quantise_h(3, 1)
                quantise_h(1, 1)
            if k == 4:
                turn_w2(0)
                turn_w2(1)
                group_w2(0)
            if k == 6:
                group_w2(1)
            if k == 8:
                quantise_w2()
            for m in range(7):
                if k == last_slot[m] + 1:
                    quantise_agg(m)
            for m in range(3, 8):
                j = k - (12 + 4 * (m - 3)) + 5
                if j in (0, 1) and 2 * j >= late_from[m]:
                    group_unit(m, 2 * j)
                    group_unit(m, 2 * j + 1)
                if j in (2, 2 + 1) and 2 * (j - 2) >= late_from[m]:
                    quantise(m, 2 * (j - 2), 2)
                if j == -4:
                    normalise(2 * m, late_from[m], CHUNKS - late_from[m])
                if j == -4 + 2:
                    normalise(2 * m + 1, late_from[m], CHUNKS - late_from[m])
            if k == len(slots) - 2:
                quantise_agg(7, 0, 2)
                project(7, (0,))
                quantise_agg(7, 2, 1)
                finish_place(7, 0)
            if k == len(slots) - 1:
                last_rows = project_last(0)
                group_agg(15, 1)
                quantise_agg(7, 3, 1)
                project_last(1)
                finish_last()
